import numpy as np
import ml_dtypes


BF16 = ml_dtypes.bfloat16


def bf(x):
    return np.asarray(x, np.float32).astype(BF16)


def f64(x):
    return np.asarray(x).astype(np.float64)


E2M1 = np.array([0.0, 0.5, 1.0, 1.5, 2.0, 3.0, 4.0, 6.0, -0.0, -0.5, -1.0, -1.5, -2.0, -3.0, -4.0, -6.0])


def pack_weight(w, fmt):
    k, n = w.shape
    w = f64(bf(w)).reshape(k // 32, 32, n)
    amax = np.abs(w).max(1)
    if fmt == "e4m3":
        byte = np.frexp(amax)[1] - 1 + 127 - 7
    else:
        mant, ex = np.frexp(amax / 6.0)
        byte = np.where(mant > 0.5, ex, ex - 1) + 127
    byte = np.clip(np.where(amax > 0, byte, 1), 1, 254)
    scaled = (w * np.exp2(127.0 - byte)[:, None, :]).reshape(k, n).astype(np.float32)
    by_word = np.ascontiguousarray(scaled.reshape(k // 512, 128, 4, n).transpose(0, 1, 3, 2))
    if fmt == "e4m3":
        words = by_word.astype(ml_dtypes.float8_e4m3fn).view(np.uint8)
    else:
        c = by_word.astype(ml_dtypes.float4_e2m1fn).view(np.uint8) & 0xF
        words = c[..., 0::2] | (c[..., 1::2] << 4)
    return np.ascontiguousarray(words), np.ascontiguousarray(byte.astype(np.uint8).reshape(k // 512, 16, n))


def unpack_weight(words, scales, fmt):
    g, p, n, _ = words.shape
    if fmt == "e4m3":
        vals = np.ascontiguousarray(words).view(ml_dtypes.float8_e4m3fn).astype(np.float64)
    else:
        nib = np.empty((g, p, n, 4), np.uint8)
        nib[..., 0::2] = words & 0xF
        nib[..., 1::2] = words >> 4
        vals = E2M1[nib]
    vals = vals * np.repeat(np.exp2(scales.astype(np.float64) - 127.0), 8, axis=1)[..., None]
    return vals.transpose(0, 1, 3, 2).reshape(g * 512, n)

def pack4(w):
    words, scales = pack_weight(w, "e2m1")
    return words.reshape(words.shape[0], 128, -1), scales


def unpack4(words, scales):
    return unpack_weight(words.reshape(words.shape[0], 128, -1, 2), scales, "e2m1")


def kspread(k):
    return np.exp2(np.repeat(np.random.randint(-6, 7, k // 32), 32).astype(np.float64))


B, S, DIM, H, HD = 4, 1024, 2048, 16, 128
E = H * HD


def rope_tables():
    inv_freq = 1.0 / (10000.0 ** (np.arange(0, HD, 2) / HD))
    freqs = np.outer(np.arange(S), inv_freq)
    emb = np.concatenate([freqs, freqs], axis=-1)
    return np.cos(emb)[None, None], np.sin(emb)[None, None]


def rotate_half(x):
    x1, x2 = np.split(x, 2, axis=-1)
    return np.concatenate([-x2, x1], axis=-1)


def setup_inputs():
    s = kspread(DIM)
    cos, sin = rope_tables()
    query = np.random.standard_normal((B, S, DIM)) * s
    query_words, query_scales = pack4(query.reshape(B * S, DIM).T)
    wq_words, wq_scales = pack4((np.random.standard_normal((E, DIM)) / np.sqrt(DIM) / s).T)
    return {"query_words": query_words, "query_scales": query_scales,
            "wq_words": wq_words, "wq_scales": wq_scales,
            "bq": bf(np.random.standard_normal(E) * 0.1),
            "cos": bf(cos), "sin": bf(sin)}


def reference(query_words, query_scales, wq_words, wq_scales, bq, cos, sin):
    q = (unpack4(query_words, query_scales).T.reshape(B, S, DIM) @ unpack4(wq_words, wq_scales)) + f64(bq)
    q = q.reshape(B, S, H, HD).transpose(0, 2, 1, 3)
    return q * f64(cos) + rotate_half(q) * f64(sin)

@@ -1,0 +1,194 @@
+from contextlib import ExitStack
+
+import concourse.mybir as mybir
+from concourse.masks import make_identity
+
+F32 = mybir.dt.float32
+BF16 = mybir.dt.bfloat16
+U8 = mybir.dt.uint8
+I32 = mybir.dt.int32
+FP4 = mybir.dt.float4_e2m1fn_x4
+ALU = mybir.AluOpType
+ACT = mybir.ActivationFunctionType
+
+B, S, DIM, H, HD = 4, 1024, 2048, 16, 128
+E = H * HD
+P = 128
+PASSES = DIM // 512
+NT = S // P
+DB = 8
+NBLK = HD // DB
+HALF = NBLK // 2
+HH = HD // 2
+BH = B * H
+FLOPS = 2 * B * S * DIM * E
+
+GP_FINAL = (0, 2, 3, 5, 6, 7)
+CT_AHEAD = 2
+CT_AT = 3
+
+
+def tile_attention_pa_kernel(tc, query_words, query_scales, wq_words, wq_scales, bq, cos, sin, out):
+    nc = tc.nc
+    with ExitStack() as ctx:
+        keep = ctx.enter_context(tc.tile_pool(name="keep", bufs=1))
+        ctp = ctx.enter_context(tc.tile_pool(name="ctp", bufs=CT_AHEAD + 1))
+        opool = ctx.enter_context(tc.tile_pool(name="opool", bufs=2))
+        work = ctx.enter_context(tc.tile_pool(name="work", bufs=6))
+        psum = ctx.enter_context(tc.psum_pool(name="psum", bufs=6))
+        psc = ctx.enter_context(tc.psum_pool(name="psc", bufs=2))
+
+        xc = keep.tile([P, PASSES, 2 * B * S], U8, align_bytes=64)
+        xs = keep.tile([P, PASSES, B * S], U8, align_bytes=64)
+        wc = keep.tile([P, PASSES, 2 * E], U8, align_bytes=64)
+        ws = keep.tile([P, PASSES, E], U8, align_bytes=64)
+        wp = keep.tile([P, PASSES, 2 * E], U8, align_bytes=64)
+        wsp = keep.tile([P, PASSES, E], U8, align_bytes=64)
+        csall = keep.tile([P, NT, 2, 2, HH], BF16)
+        cf = keep.tile([P, NT, HD], F32)
+        sg = keep.tile([P, NT, HD], F32)
+        lt = keep.tile([P, NT, 2, P], BF16)
+        rr = keep.tile([P, 2, HH, H], BF16)
+        ident = keep.tile([P, P], BF16)
+        mask = keep.tile([P, HH], BF16)
+        brow = keep.tile([P, 2, P], BF16)
+        bk = keep.tile([P, 2, H], BF16)
+
+        nc.vector.memset(ws[:].bitcast(I32), 0)
+        nc.vector.memset(xs[:, 0:2, :].bitcast(I32), 0)
+        nc.gpsimd.memset(xs[:, 2:4, :].bitcast(F32), 0.0)
+        nc.vector.memset(brow[:], 0.0)
+        for g in range(PASSES):
+            nc.sync.dma_start(out=wc[:, g, :].bitcast(I32), in_=wq_words[g].bitcast(I32))
+        for q in range(4):
+            nc.sync.dma_start(
+                out=ws[32 * q : 32 * q + 4, :, :].bitcast(I32),
+                in_=wq_scales[:, 4 * q : 4 * q + 4, :].rearrange("g r n -> r g n").bitcast(I32),
+            )
+        xc_v = xc[:].rearrange("p g (b w) -> p g b w", b=B)
+        qw_v = query_words.rearrange("g p (b w) -> g p b w", b=B)
+        for g in range(PASSES):
+            nc.sync.dma_start(out=xc_v[:, g, :, 0:256].bitcast(I32), in_=qw_v[g, :, :, 0:256].bitcast(I32))
+        for q in range(4):
+            nc.sync.dma_start(
+                out=xs[32 * q : 32 * q + 4, :, :].bitcast(I32),
+                in_=query_scales[:, 4 * q : 4 * q + 4, :].rearrange("g r n -> r g n").bitcast(I32),
+            )
+        for g in range(PASSES):
+            nc.sync.dma_start(out=xc_v[:, g, :, 256:2048].bitcast(I32), in_=qw_v[g, :, :, 256:2048].bitcast(I32))
+        cos_v = cos.rearrange("a b (i p) d -> p (a b i) d", p=P)
+        sin_v = sin.rearrange("a b (i p) d -> p (a b i) d", p=P)
+        bq_hd = bq.rearrange("(h d) -> h d", h=H)
+        for u in range(2):
+            nc.scalar.dma_start(out=csall[:, :, u, 0, :], in_=cos_v[:, :, HH * u : HH * (u + 1)])
+            nc.scalar.dma_start(out=csall[:, :, u, 1, :], in_=sin_v[:, :, HH * u : HH * (u + 1)])
+        nc.scalar.dma_start(out=brow[0:H, 0, :], in_=bq_hd)
+        nc.scalar.dma_start(out=brow[0:H, 1, 0:HH], in_=bq_hd[:, HH:HD])
+        nc.scalar.dma_start(out=brow[0:H, 1, HH:HD], in_=bq_hd[:, 0:HH])
+
+        make_identity(nc, ident[:])
+        nc.vector.tensor_tensor(out=mask[:], in0=ident[:, 0:HH], in1=ident[:, HH:P], op=ALU.add)
+        nc.vector.tensor_scalar(out=csall[:, :, 0, 1, :], in0=csall[:, :, 0, 1, :], scalar1=-1.0, scalar2=None, op0=ALU.mult)
+        nc.vector.tensor_copy(out=cf[:].rearrange("p i (u d) -> p i u d", u=2), in_=csall[:, :, :, 0, :])
+        nc.vector.tensor_copy(out=sg[:].rearrange("p i (u d) -> p i u d", u=2), in_=csall[:, :, :, 1, :])
+        bt = psc.tile([P, 2, P], BF16, name="cps")
+        for u in range(2):
+            nc.tensor.transpose(bt[:, u, :], brow[:, u, :], ident[:])
+        nc.vector.tensor_copy(out=bk[:], in_=bt[:, :, 0:H])
+        for u in range(2):
+            nc.vector.tensor_tensor(
+                out=rr[:, u], in0=mask[:].unsqueeze(2).to_broadcast([P, HH, H]),
+                in1=bk[:, u, :].unsqueeze(1).to_broadcast([P, HH, H]), op=ALU.mult,
+            )
+        for i0 in range(0, NT, 2):
+            tp = psc.tile([P, 4, P], BF16, name="cps")
+            for j in range(4):
+                nc.tensor.transpose(tp[:, j, :], csall[:, i0 + j // 2, j % 2].rearrange("p k d -> p (k d)"), ident[:])
+            nc.vector.tensor_copy(out=lt[:, i0 : i0 + 2].rearrange("p i u t -> p (i u) t"), in_=tp[:])
+
+        def ctab(i):
+            ct = ctp.tile([P, HD, H], F32, name="ct")
+            for u in range(2):
+                for v in range(2):
+                    cp = psc.tile([P, 32, H], F32, name="cps")
+                    nc.tensor.matmul(
+                        out=cp[:].rearrange("p d h -> p (d h)"), lhsT=lt[:, i, u, :],
+                        rhs=rr[:, u, 32 * v : 32 * v + 32, :].rearrange("p d h -> p (d h)"), start=True, stop=True,
+                    )
+                    d0 = HH * u + 32 * v
+                    nc.scalar.copy(out=ct[:, d0 : d0 + 32, :], in_=cp[:])
+            return ct
+
+        cts = [ctab(i) for i in range(CT_AHEAD)]
+
+        wc_v = wc[:].bitcast(I32).rearrange("p g (h c w) -> p g c h w", h=H, c=NBLK)
+        wp_v = wp[:].bitcast(I32).rearrange("p g (c h w) -> p g c h w", c=NBLK, h=H)
+        ws_v = ws[:].bitcast(I32).rearrange("p g (h c w) -> p g c h w", h=H, c=NBLK)
+        wsp_v = wsp[:].bitcast(I32).rearrange("p g (c h w) -> p g c h w", c=NBLK, h=H)
+        for c0 in range(HALF):
+            for c in (c0, c0 + HALF):
+                nc.vector.tensor_copy(out=wsp_v[:, :, c], in_=ws_v[:, :, c])
+                nc.vector.tensor_copy(out=wp_v[:, :, c], in_=wc_v[:, :, c])
+
+        def fill_bank(i, c):
+            acc = psum.tile([P, B, H, DB], F32, name="acc")
+            for b in range(B):
+                t0 = b * S + i * P
+                for g in range(PASSES):
+                    nc.tensor.matmul_mx(
+                        out=acc[:, b].rearrange("p h e -> p (h e)"),
+                        lhsT=xc[:, g, 2 * t0 : 2 * t0 + 256].bitcast(FP4),
+                        lhsT_scale=xs[:, g, t0 : t0 + P],
+                        rhs=wp[:, g, 256 * c : 256 * c + 256].bitcast(FP4),
+                        rhs_scale=wsp[:, g, P * c : P * c + P],
+                        start=(g == 0),
+                        stop=(g == PASSES - 1),
+                    )
+            return acc
+
+        def cos_part(acc, i, c):
+            x = work.tile([P, DB, B, H], F32, name="x")
+            for e in range(DB):
+                d = DB * c + e
+                nc.scalar.activation(out=x[:, e], in_=acc[:, :, :, e], func=ACT.Copy, scale=cf[:, i, d : d + 1])
+            return x
+
+        def sin_part(acc, ct, i, c):
+            y = work.tile([P, DB, B, H], F32, name="y")
+            cp = (c + HALF) % NBLK
+            for e in range(DB):
+                d = DB * cp + e
+                nc.vector.scalar_tensor_tensor(
+                    out=y[:, e], in0=acc[:, :, :, e], scalar=sg[:, i, d : d + 1],
+                    in1=ct[:, d, :].unsqueeze(1).to_broadcast([P, B, H]), op0=ALU.mult, op1=ALU.add,
+                )
+            return y
+
+        def final(eng, o, x, y, c):
+            for u in range(2):
+                d0 = DB * c + 4 * u
+                eng.tensor_tensor(
+                    out=o[:, :, d0 : d0 + 4].rearrange("p (a l) e -> p a l e", l=4),
+                    in0=x[:, 4 * u : 4 * u + 4].rearrange("p e b h -> p e (b h)").rearrange("p e (a l) -> p a l e", l=4),
+                    in1=y[:, 4 * u : 4 * u + 4].rearrange("p e b h -> p e (b h)").rearrange("p e (a l) -> p a l e", l=4),
+                    op=ALU.add,
+                )
+
+        for i in range(NT):
+            ct = cts[i]
+            o = opool.tile([P, BH, HD], F32, name="o")
+            for c in range(HALF):
+                acc_a = fill_bank(i, c)
+                acc_b = fill_bank(i, c + HALF)
+                if c == CT_AT and i + CT_AHEAD < NT:
+                    cts.append(ctab(i + CT_AHEAD))
+                x_a = cos_part(acc_a, i, c)
+                x_b = cos_part(acc_b, i, c + HALF)
+                y_hi = sin_part(acc_a, ct, i, c)
+                y_lo = sin_part(acc_b, ct, i, c + HALF)
+                final(nc.vector, o, x_a, y_lo, c)
+                final(nc.gpsimd if c in GP_FINAL else nc.vector, o, x_b, y_hi, c + HALF)
+            for b in range(B):
+                nc.sync.dma_start(
+                    out=out[b, :, P * i : P * (i + 1), :].rearrange("h p d -> p h d"), in_=o[:, H * b : H * (b + 1), :]
+                )

@@ -23,9 +23,10 @@ HH = HD // 2
 BH = B * H
 FLOPS = 2 * B * S * DIM * E
 
-GP_FINAL = (0, 2, 3, 5, 6, 7)
+CHAIN_PAIRS = (5,)
 CT_AHEAD = 2
-CT_AT = 3
+CT_AT = 2
+VEC_TAIL = 2
 
 
 def tile_attention_pa_kernel(tc, query_words, query_scales, wq_words, wq_scales, bq, cos, sin, out):
@@ -33,17 +34,15 @@ def tile_attention_pa_kernel(tc, query_words, query_scales, wq_words, wq_scales,
     with ExitStack() as ctx:
         keep = ctx.enter_context(tc.tile_pool(name="keep", bufs=1))
         ctp = ctx.enter_context(tc.tile_pool(name="ctp", bufs=CT_AHEAD + 1))
-        opool = ctx.enter_context(tc.tile_pool(name="opool", bufs=2))
-        work = ctx.enter_context(tc.tile_pool(name="work", bufs=6))
         psum = ctx.enter_context(tc.psum_pool(name="psum", bufs=6))
         psc = ctx.enter_context(tc.psum_pool(name="psc", bufs=2))
 
         xc = keep.tile([P, PASSES, 2 * B * S], U8, align_bytes=64)
         xs = keep.tile([P, PASSES, B * S], U8, align_bytes=64)
-        wc = keep.tile([P, PASSES, 2 * E], U8, align_bytes=64)
-        ws = keep.tile([P, PASSES, E], U8, align_bytes=64)
         wp = keep.tile([P, PASSES, 2 * E], U8, align_bytes=64)
         wsp = keep.tile([P, PASSES, E], U8, align_bytes=64)
+        cs = keep.tile([P, NT, HD], BF16)
+        sn = keep.tile([P, NT, HD], BF16)
         csall = keep.tile([P, NT, 2, 2, HH], BF16)
         cf = keep.tile([P, NT, HD], F32)
         sg = keep.tile([P, NT, HD], F32)
@@ -53,58 +52,6 @@ def tile_attention_pa_kernel(tc, query_words, query_scales, wq_words, wq_scales,
         mask = keep.tile([P, HH], BF16)
         brow = keep.tile([P, 2, P], BF16)
         bk = keep.tile([P, 2, H], BF16)
-
-        nc.vector.memset(ws[:].bitcast(I32), 0)
-        nc.vector.memset(xs[:, 0:2, :].bitcast(I32), 0)
-        nc.gpsimd.memset(xs[:, 2:4, :].bitcast(F32), 0.0)
-        nc.vector.memset(brow[:], 0.0)
-        for g in range(PASSES):
-            nc.sync.dma_start(out=wc[:, g, :].bitcast(I32), in_=wq_words[g].bitcast(I32))
-        for q in range(4):
-            nc.sync.dma_start(
-                out=ws[32 * q : 32 * q + 4, :, :].bitcast(I32),
-                in_=wq_scales[:, 4 * q : 4 * q + 4, :].rearrange("g r n -> r g n").bitcast(I32),
-            )
-        xc_v = xc[:].rearrange("p g (b w) -> p g b w", b=B)
-        qw_v = query_words.rearrange("g p (b w) -> g p b w", b=B)
-        for g in range(PASSES):
-            nc.sync.dma_start(out=xc_v[:, g, :, 0:256].bitcast(I32), in_=qw_v[g, :, :, 0:256].bitcast(I32))
-        for q in range(4):
-            nc.sync.dma_start(
-                out=xs[32 * q : 32 * q + 4, :, :].bitcast(I32),
-                in_=query_scales[:, 4 * q : 4 * q + 4, :].rearrange("g r n -> r g n").bitcast(I32),
-            )
-        for g in range(PASSES):
-            nc.sync.dma_start(out=xc_v[:, g, :, 256:2048].bitcast(I32), in_=qw_v[g, :, :, 256:2048].bitcast(I32))
-        cos_v = cos.rearrange("a b (i p) d -> p (a b i) d", p=P)
-        sin_v = sin.rearrange("a b (i p) d -> p (a b i) d", p=P)
-        bq_hd = bq.rearrange("(h d) -> h d", h=H)
-        for u in range(2):
-            nc.scalar.dma_start(out=csall[:, :, u, 0, :], in_=cos_v[:, :, HH * u : HH * (u + 1)])
-            nc.scalar.dma_start(out=csall[:, :, u, 1, :], in_=sin_v[:, :, HH * u : HH * (u + 1)])
-        nc.scalar.dma_start(out=brow[0:H, 0, :], in_=bq_hd)
-        nc.scalar.dma_start(out=brow[0:H, 1, 0:HH], in_=bq_hd[:, HH:HD])
-        nc.scalar.dma_start(out=brow[0:H, 1, HH:HD], in_=bq_hd[:, 0:HH])
-
-        make_identity(nc, ident[:])
-        nc.vector.tensor_tensor(out=mask[:], in0=ident[:, 0:HH], in1=ident[:, HH:P], op=ALU.add)
-        nc.vector.tensor_scalar(out=csall[:, :, 0, 1, :], in0=csall[:, :, 0, 1, :], scalar1=-1.0, scalar2=None, op0=ALU.mult)
-        nc.vector.tensor_copy(out=cf[:].rearrange("p i (u d) -> p i u d", u=2), in_=csall[:, :, :, 0, :])
-        nc.vector.tensor_copy(out=sg[:].rearrange("p i (u d) -> p i u d", u=2), in_=csall[:, :, :, 1, :])
-        bt = psc.tile([P, 2, P], BF16, name="cps")
-        for u in range(2):
-            nc.tensor.transpose(bt[:, u, :], brow[:, u, :], ident[:])
-        nc.vector.tensor_copy(out=bk[:], in_=bt[:, :, 0:H])
-        for u in range(2):
-            nc.vector.tensor_tensor(
-                out=rr[:, u], in0=mask[:].unsqueeze(2).to_broadcast([P, HH, H]),
-                in1=bk[:, u, :].unsqueeze(1).to_broadcast([P, HH, H]), op=ALU.mult,
-            )
-        for i0 in range(0, NT, 2):
-            tp = psc.tile([P, 4, P], BF16, name="cps")
-            for j in range(4):
-                nc.tensor.transpose(tp[:, j, :], csall[:, i0 + j // 2, j % 2].rearrange("p k d -> p (k d)"), ident[:])
-            nc.vector.tensor_copy(out=lt[:, i0 : i0 + 2].rearrange("p i u t -> p (i u) t"), in_=tp[:])
 
         def ctab(i):
             ct = ctp.tile([P, HD, H], F32, name="ct")
@@ -119,24 +66,84 @@ def tile_attention_pa_kernel(tc, query_words, query_scales, wq_words, wq_scales,
                     nc.scalar.copy(out=ct[:, d0 : d0 + 32, :], in_=cp[:])
             return ct
 
-        cts = [ctab(i) for i in range(CT_AHEAD)]
+        with tc.tile_pool(name="stage", bufs=1) as stage:
+            wc = stage.tile([P, PASSES, 2 * E], U8, align_bytes=64)
+            ws = stage.tile([P, PASSES, E], U8, align_bytes=64)
 
-        wc_v = wc[:].bitcast(I32).rearrange("p g (h c w) -> p g c h w", h=H, c=NBLK)
-        wp_v = wp[:].bitcast(I32).rearrange("p g (c h w) -> p g c h w", c=NBLK, h=H)
-        ws_v = ws[:].bitcast(I32).rearrange("p g (h c w) -> p g c h w", h=H, c=NBLK)
-        wsp_v = wsp[:].bitcast(I32).rearrange("p g (c h w) -> p g c h w", c=NBLK, h=H)
-        for c0 in range(HALF):
-            for c in (c0, c0 + HALF):
-                nc.vector.tensor_copy(out=wsp_v[:, :, c], in_=ws_v[:, :, c])
-                nc.vector.tensor_copy(out=wp_v[:, :, c], in_=wc_v[:, :, c])
+            nc.vector.memset(brow[:, 0, :], 0.0)
+            nc.gpsimd.dma_start(out=cs[:], in_=cos.rearrange("a b (i p) d -> p (a b i) d", p=P))
+            nc.gpsimd.dma_start(out=sn[:], in_=sin.rearrange("a b (i p) d -> p (a b i) d", p=P))
+            nc.gpsimd.dma_start(out=brow[0:H, 0, :], in_=bq.rearrange("(h d) -> h d", h=H))
+            nc.vector.memset(ws[:].bitcast(I32), 0)
+            nc.vector.memset(xs[:, 0:2, :].bitcast(I32), 0)
+            nc.gpsimd.memset(xs[:, 2:4, :].bitcast(F32), 0.0)
+            for g0 in range(0, PASSES, 2):
+                nc.sync.dma_start(
+                    out=wc[:, g0 : g0 + 2, :].bitcast(I32), in_=wq_words[g0 : g0 + 2].rearrange("g p n -> p g n").bitcast(I32)
+                )
+            for q in range(4):
+                nc.sync.dma_start(
+                    out=ws[32 * q : 32 * q + 4, :, :].bitcast(I32),
+                    in_=wq_scales[:, 4 * q : 4 * q + 4, :].rearrange("g r n -> r g n").bitcast(I32),
+                )
+            xc_v = xc[:].rearrange("p g (b w) -> p g b w", b=B)
+            qw_v = query_words.rearrange("g p (b w) -> g p b w", b=B)
+            for g in range(PASSES):
+                nc.sync.dma_start(out=xc_v[:, g, :, 0:256].bitcast(I32), in_=qw_v[g, :, :, 0:256].bitcast(I32))
+            for q in range(4):
+                nc.sync.dma_start(
+                    out=xs[32 * q : 32 * q + 4, :, :].bitcast(I32),
+                    in_=query_scales[:, 4 * q : 4 * q + 4, :].rearrange("g r n -> r g n").bitcast(I32),
+                )
+            for g in range(PASSES):
+                nc.sync.dma_start(out=xc_v[:, g, :, 256:2048].bitcast(I32), in_=qw_v[g, :, :, 256:2048].bitcast(I32))
 
-        def fill_bank(i, c):
-            acc = psum.tile([P, B, H, DB], F32, name="acc")
-            for b in range(B):
-                t0 = b * S + i * P
+            make_identity(nc, ident[:])
+            nc.vector.tensor_tensor(out=mask[:], in0=ident[:, 0:HH], in1=ident[:, HH:P], op=ALU.add)
+            cs_v = cs[:].rearrange("p i (u d) -> p i u d", u=2)
+            sn_v = sn[:].rearrange("p i (u d) -> p i u d", u=2)
+            nc.vector.tensor_copy(out=csall[:, :, :, 0, :], in_=cs_v)
+            nc.vector.tensor_scalar(out=csall[:, :, 0, 1, :], in0=sn_v[:, :, 0, :], scalar1=-1.0, scalar2=None, op0=ALU.mult)
+            nc.vector.tensor_copy(out=csall[:, :, 1, 1, :], in_=sn_v[:, :, 1, :])
+            nc.vector.tensor_copy(out=brow[:, 1, 0:HH], in_=brow[:, 0, HH:HD])
+            nc.vector.tensor_copy(out=brow[:, 1, HH:HD], in_=brow[:, 0, 0:HH])
+            bt = psc.tile([P, 2, P], BF16, name="cps")
+            for u in range(2):
+                nc.tensor.transpose(bt[:, u, :], brow[:, u, :], ident[:])
+            nc.vector.tensor_copy(out=bk[:], in_=bt[:, :, 0:H])
+            for u in range(2):
+                nc.vector.tensor_tensor(
+                    out=rr[:, u], in0=mask[:].unsqueeze(2).to_broadcast([P, HH, H]),
+                    in1=bk[:, u, :].unsqueeze(1).to_broadcast([P, HH, H]), op=ALU.mult,
+                )
+            for i0 in range(0, NT, 2):
+                tp = psc.tile([P, 4, P], BF16, name="cps")
+                for j in range(4):
+                    nc.tensor.transpose(tp[:, j, :], csall[:, i0 + j // 2, j % 2].rearrange("p k d -> p (k d)"), ident[:])
+                nc.vector.tensor_copy(out=lt[:, i0 : i0 + 2].rearrange("p i u t -> p (i u) t"), in_=tp[:])
+            nc.vector.tensor_copy(out=cf[:], in_=cs[:])
+            nc.vector.tensor_copy(out=sg[:].rearrange("p i (u d) -> p i u d", u=2), in_=csall[:, :, :, 1, :])
+
+            cts = [ctab(i) for i in range(CT_AHEAD)]
+
+            wc_v = wc[:].bitcast(I32).rearrange("p g (h c w) -> p g c h w", h=H, c=NBLK)
+            wp_v = wp[:].bitcast(I32).rearrange("p g (c h w) -> p g c h w", c=NBLK, h=H)
+            ws_v = ws[:].bitcast(I32).rearrange("p g (h c w) -> p g c h w", h=H, c=NBLK)
+            wsp_v = wsp[:].bitcast(I32).rearrange("p g (c h w) -> p g c h w", c=NBLK, h=H)
+            for c0 in range(HALF):
+                for c in (c0, c0 + HALF):
+                    nc.vector.tensor_copy(out=wsp_v[:, :, c], in_=ws_v[:, :, c])
+                    nc.vector.tensor_copy(out=wp_v[:, :, c], in_=wc_v[:, :, c])
+
+        opool = ctx.enter_context(tc.tile_pool(name="opool", bufs=2))
+        work = ctx.enter_context(tc.tile_pool(name="work", bufs=4))
+
+        def fill(view, i, c, b0, nb):
+            for j in range(nb):
+                t0 = (b0 + j) * S + i * P
                 for g in range(PASSES):
                     nc.tensor.matmul_mx(
-                        out=acc[:, b].rearrange("p h e -> p (h e)"),
+                        out=view[:, j].rearrange("p h e -> p (h e)"),
                         lhsT=xc[:, g, 2 * t0 : 2 * t0 + 256].bitcast(FP4),
                         lhsT_scale=xs[:, g, t0 : t0 + P],
                         rhs=wp[:, g, 256 * c : 256 * c + 256].bitcast(FP4),
@@ -144,51 +151,70 @@ def tile_attention_pa_kernel(tc, query_words, query_scales, wq_words, wq_scales,
                         start=(g == 0),
                         stop=(g == PASSES - 1),
                     )
-            return acc
 
-        def cos_part(acc, i, c):
-            x = work.tile([P, DB, B, H], F32, name="x")
-            for e in range(DB):
-                d = DB * c + e
-                nc.scalar.activation(out=x[:, e], in_=acc[:, :, :, e], func=ACT.Copy, scale=cf[:, i, d : d + 1])
-            return x
-
-        def sin_part(acc, ct, i, c):
-            y = work.tile([P, DB, B, H], F32, name="y")
-            cp = (c + HALF) % NBLK
-            for e in range(DB):
-                d = DB * cp + e
-                nc.vector.scalar_tensor_tensor(
-                    out=y[:, e], in0=acc[:, :, :, e], scalar=sg[:, i, d : d + 1],
-                    in1=ct[:, d, :].unsqueeze(1).to_broadcast([P, B, H]), op0=ALU.mult, op1=ALU.add,
-                )
-            return y
-
-        def final(eng, o, x, y, c):
-            for u in range(2):
-                d0 = DB * c + 4 * u
+        def pair(i, c, b0, nb, o, ct, last):
+            if nb == B:
+                acc_lo = psum.tile([P, nb, H, DB], F32, name="acc")
+                acc_hi = psum.tile([P, nb, H, DB], F32, name="acc")
+                accs = (acc_lo[:], acc_hi[:])
+            else:
+                acc2 = psum.tile([P, 2, nb, H, DB], F32, name="acc")
+                accs = (acc2[:, 0], acc2[:, 1])
+            for s in range(2):
+                fill(accs[s], i, c + HALF * s, b0, nb)
+            if c == CT_AT and b0 == 0 and i + CT_AHEAD < NT:
+                cts.append(ctab(i + CT_AHEAD))
+            x = work.tile([P, 2, DB, nb, H], F32, name="x")
+            y = work.tile([P, 2, DB, nb, H], F32, name="y")
+            n0, nn = H * b0, H * nb
+            chain = c in CHAIN_PAIRS
+            for s in range(2):
+                for e in range(DB):
+                    d = DB * (c + HALF * s) + e
+                    if chain:
+                        nc.vector.scalar_tensor_tensor(
+                            out=x[:, s, e], in0=accs[s][:, :, :, e], scalar=cf[:, i, d : d + 1],
+                            in1=ct[:, d, :].unsqueeze(1).to_broadcast([P, nb, H]), op0=ALU.mult, op1=ALU.add,
+                        )
+                    else:
+                        nc.scalar.activation(out=x[:, s, e], in_=accs[s][:, :, :, e], func=ACT.Copy, scale=cf[:, i, d : d + 1])
+            for t in range(2):
+                s = 1 - t
+                for e in range(DB):
+                    d = DB * (c + HALF * s) + e
+                    nc.vector.scalar_tensor_tensor(
+                        out=y[:, s, e], in0=accs[t][:, :, :, e], scalar=sg[:, i, d : d + 1],
+                        in1=(x[:, s, e] if chain else ct[:, d, :].unsqueeze(1).to_broadcast([P, nb, H])),
+                        op0=ALU.mult, op1=ALU.add,
+                    )
+            if chain:
+                for s in range(2):
+                    for u in range(2):
+                        d0 = DB * (c + HALF * s) + 4 * u
+                        nc.scalar.copy(
+                            out=o[:, n0 : n0 + nn, d0 : d0 + 4].rearrange("p (a l) e -> p a l e", l=4),
+                            in_=y[:, s, 4 * u : 4 * u + 4].rearrange("p e b h -> p e (b h)").rearrange("p e (a l) -> p a l e", l=4),
+                        )
+            else:
+                eng = nc.vector if last else nc.gpsimd
                 eng.tensor_tensor(
-                    out=o[:, :, d0 : d0 + 4].rearrange("p (a l) e -> p a l e", l=4),
-                    in0=x[:, 4 * u : 4 * u + 4].rearrange("p e b h -> p e (b h)").rearrange("p e (a l) -> p a l e", l=4),
-                    in1=y[:, 4 * u : 4 * u + 4].rearrange("p e b h -> p e (b h)").rearrange("p e (a l) -> p a l e", l=4),
+                    out=o[:, n0 : n0 + nn, :].rearrange("p n (s c e) -> p s c n e", s=2, c=HALF)[:, :, c],
+                    in0=x[:].rearrange("p s e b h -> p s (b h) e"),
+                    in1=y[:].rearrange("p s e b h -> p s (b h) e"),
                     op=ALU.add,
                 )
 
+        def store(o, i, b):
+            nc.sync.dma_start(
+                out=out[b, :, P * i : P * (i + 1), :].rearrange("h p d -> p h d"), in_=o[:, H * b : H * (b + 1), :]
+            )
+
         for i in range(NT):
-            ct = cts[i]
             o = opool.tile([P, BH, HD], F32, name="o")
-            for c in range(HALF):
-                acc_a = fill_bank(i, c)
-                acc_b = fill_bank(i, c + HALF)
-                if c == CT_AT and i + CT_AHEAD < NT:
-                    cts.append(ctab(i + CT_AHEAD))
-                x_a = cos_part(acc_a, i, c)
-                x_b = cos_part(acc_b, i, c + HALF)
-                y_hi = sin_part(acc_a, ct, i, c)
-                y_lo = sin_part(acc_b, ct, i, c + HALF)
-                final(nc.vector, o, x_a, y_lo, c)
-                final(nc.gpsimd if c in GP_FINAL else nc.vector, o, x_b, y_hi, c + HALF)
-            for b in range(B):
-                nc.sync.dma_start(
-                    out=out[b, :, P * i : P * (i + 1), :].rearrange("h p d -> p h d"), in_=o[:, H * b : H * (b + 1), :]
-                )
+            nb = B // 2 if i == NT - 1 else B
+            for b0 in range(0, B, nb):
+                for c in range(HALF):
+                    last = i == NT - 1 and b0 + nb == B and c >= HALF - VEC_TAIL
+                    pair(i, c, b0, nb, o, cts[i], last)
+                for b in range(b0, b0 + nb):
+                    store(o, i, b)

@@ -23,7 +23,8 @@ HH = HD // 2
 BH = B * H
 FLOPS = 2 * B * S * DIM * E
 
-CHAIN_PAIRS = (5,)
+KINDS = ("G", "C", "D", "G", "C", "D", "G", "C")
+LAG = 3
 CT_AHEAD = 2
 CT_AT = 2
 VEC_TAIL = 2
@@ -152,7 +153,14 @@ def tile_attention_pa_kernel(tc, query_words, query_scales, wq_words, wq_scales,
                         stop=(g == PASSES - 1),
                     )
 
-        def pair(i, c, b0, nb, o, ct, last):
+        def o_quad(o, n0, nn, c, s, u):
+            d0 = DB * (c + HALF * s) + 4 * u
+            return o[:, n0 : n0 + nn, d0 : d0 + 4].rearrange("p (a l) e -> p a l e", l=4)
+
+        def t_quad(t, s, u):
+            return t[:, s, 4 * u : 4 * u + 4].rearrange("p e b h -> p e (b h)").rearrange("p e (a l) -> p a l e", l=4)
+
+        def pair_main(i, c, b0, nb, o, ct, kind):
             if nb == B:
                 acc_lo = psum.tile([P, nb, H, DB], F32, name="acc")
                 acc_hi = psum.tile([P, nb, H, DB], F32, name="acc")
@@ -164,10 +172,10 @@ def tile_attention_pa_kernel(tc, query_words, query_scales, wq_words, wq_scales,
                 fill(accs[s], i, c + HALF * s, b0, nb)
             if c == CT_AT and b0 == 0 and i + CT_AHEAD < NT:
                 cts.append(ctab(i + CT_AHEAD))
-            x = work.tile([P, 2, DB, nb, H], F32, name="x")
-            y = work.tile([P, 2, DB, nb, H], F32, name="y")
+            x = work.tile([P, 2, DB, nb, H], F32, name="x", bufs=4)
+            y = work.tile([P, 2, DB, nb, H], F32, name="y", bufs=7)
             n0, nn = H * b0, H * nb
-            chain = c in CHAIN_PAIRS
+            chain = kind == "C"
             for s in range(2):
                 for e in range(DB):
                     d = DB * (c + HALF * s) + e
@@ -188,33 +196,48 @@ def tile_attention_pa_kernel(tc, query_words, query_scales, wq_words, wq_scales,
                         op0=ALU.mult, op1=ALU.add,
                     )
             if chain:
-                for s in range(2):
-                    for u in range(2):
-                        d0 = DB * (c + HALF * s) + 4 * u
-                        nc.scalar.copy(
-                            out=o[:, n0 : n0 + nn, d0 : d0 + 4].rearrange("p (a l) e -> p a l e", l=4),
-                            in_=y[:, s, 4 * u : 4 * u + 4].rearrange("p e b h -> p e (b h)").rearrange("p e (a l) -> p a l e", l=4),
-                        )
-            else:
-                eng = nc.vector if last else nc.gpsimd
-                eng.tensor_tensor(
-                    out=o[:, n0 : n0 + nn, :].rearrange("p n (s c e) -> p s c n e", s=2, c=HALF)[:, :, c],
-                    in0=x[:].rearrange("p s e b h -> p s (b h) e"),
-                    in1=y[:].rearrange("p s e b h -> p s (b h) e"),
-                    op=ALU.add,
-                )
+                return y
+            if kind == "G":
+                flat = "p s e b h -> p (s e b h)"
+                nc.gpsimd.tensor_tensor(out=y[:].rearrange(flat), in0=x[:].rearrange(flat), in1=y[:].rearrange(flat), op=ALU.add)
+                return y
+            eng = nc.vector if kind == "V" else nc.gpsimd
+            for s in range(2):
+                for u in range(2):
+                    eng.tensor_tensor(out=o_quad(o, n0, nn, c, s, u), in0=t_quad(x, s, u), in1=t_quad(y, s, u), op=ALU.add)
+            return None
+
+        def unpermute(o, t, c, b0, nb):
+            for s in range(2):
+                for u in range(2):
+                    nc.scalar.copy(out=o_quad(o, H * b0, H * nb, c, s, u), in_=t_quad(t, s, u))
 
         def store(o, i, b):
             nc.sync.dma_start(
                 out=out[b, :, P * i : P * (i + 1), :].rearrange("h p d -> p h d"), in_=o[:, H * b : H * (b + 1), :]
             )
 
+        jobs = []
         for i in range(NT):
-            o = opool.tile([P, BH, HD], F32, name="o")
             nb = B // 2 if i == NT - 1 else B
             for b0 in range(0, B, nb):
                 for c in range(HALF):
-                    last = i == NT - 1 and b0 + nb == B and c >= HALF - VEC_TAIL
-                    pair(i, c, b0, nb, o, cts[i], last)
-                for b in range(b0, b0 + nb):
-                    store(o, i, b)
+                    jobs.append((i, b0, nb, c))
+        outs = {}
+        left = []
+        with tc.manual_schedule():
+            for k in range(len(jobs) + LAG):
+                if k < len(jobs):
+                    i, b0, nb, c = jobs[k]
+                    if (b0, c) == (0, 0):
+                        o_new = opool.tile([P, BH, HD], F32, name="o")
+                        outs[i] = o_new
+                    kind = "V" if k >= len(jobs) - VEC_TAIL else KINDS[c]
+                    left.append(pair_main(i, c, b0, nb, outs[i], cts[i], kind))
+                if k >= LAG:
+                    i, b0, nb, c = jobs[k - LAG]
+                    if left[k - LAG] is not None:
+                        unpermute(outs[i], left[k - LAG], c, b0, nb)
+                    if c == HALF - 1:
+                        for b in range(b0, b0 + nb):
+                            store(outs[i], i, b)

@@ -23,8 +23,8 @@ HH = HD // 2
 BH = B * H
 FLOPS = 2 * B * S * DIM * E
 
-KINDS = ("G", "C", "D", "G", "C", "D", "G", "C")
-LAG = 3
+KINDS = ("G", "D", "G", "D", "C", "G", "D", "G")
+LAG = 4
 CT_AHEAD = 2
 CT_AT = 2
 VEC_TAIL = 2
@@ -76,8 +76,7 @@ def tile_attention_pa_kernel(tc, query_words, query_scales, wq_words, wq_scales,
             nc.gpsimd.dma_start(out=sn[:], in_=sin.rearrange("a b (i p) d -> p (a b i) d", p=P))
             nc.gpsimd.dma_start(out=brow[0:H, 0, :], in_=bq.rearrange("(h d) -> h d", h=H))
             nc.vector.memset(ws[:].bitcast(I32), 0)
-            nc.vector.memset(xs[:, 0:2, :].bitcast(I32), 0)
-            nc.gpsimd.memset(xs[:, 2:4, :].bitcast(F32), 0.0)
+            nc.vector.memset(xs[:].bitcast(I32), 0)
             for g0 in range(0, PASSES, 2):
                 nc.sync.dma_start(
                     out=wc[:, g0 : g0 + 2, :].bitcast(I32), in_=wq_words[g0 : g0 + 2].rearrange("g p n -> p g n").bitcast(I32)
@@ -173,7 +172,7 @@ def tile_attention_pa_kernel(tc, query_words, query_scales, wq_words, wq_scales,
             if c == CT_AT and b0 == 0 and i + CT_AHEAD < NT:
                 cts.append(ctab(i + CT_AHEAD))
             x = work.tile([P, 2, DB, nb, H], F32, name="x", bufs=4)
-            y = work.tile([P, 2, DB, nb, H], F32, name="y", bufs=7)
+            y = work.tile([P, 2, DB, nb, H], F32, name="y", bufs=8)
             n0, nn = H * b0, H * nb
             chain = kind == "C"
             for s in range(2):

@@ -23,7 +23,7 @@ HH = HD // 2
 BH = B * H
 FLOPS = 2 * B * S * DIM * E
 
-KINDS = ("G", "D", "G", "D", "C", "G", "D", "G")
+KINDS = (("G", "D", "C", "G", "G", "D", "C", "G"), ("G", "D", "C", "G", "G", "G", "C", "G"))
 LAG = 4
 CT_AHEAD = 2
 CT_AT = 2
@@ -171,8 +171,8 @@ def tile_attention_pa_kernel(tc, query_words, query_scales, wq_words, wq_scales,
                 fill(accs[s], i, c + HALF * s, b0, nb)
             if c == CT_AT and b0 == 0 and i + CT_AHEAD < NT:
                 cts.append(ctab(i + CT_AHEAD))
-            x = work.tile([P, 2, DB, nb, H], F32, name="x", bufs=4)
-            y = work.tile([P, 2, DB, nb, H], F32, name="y", bufs=8)
+            x = work.tile([P, 2, DB, nb, H], F32, name="x", bufs=5)
+            y = work.tile([P, 2, DB, nb, H], F32, name="y", bufs=7)
             n0, nn = H * b0, H * nb
             chain = kind == "C"
             for s in range(2):
@@ -231,7 +231,7 @@ def tile_attention_pa_kernel(tc, query_words, query_scales, wq_words, wq_scales,
                     if (b0, c) == (0, 0):
                         o_new = opool.tile([P, BH, HD], F32, name="o")
                         outs[i] = o_new
-                    kind = "V" if k >= len(jobs) - VEC_TAIL else KINDS[c]
+                    kind = "V" if k >= len(jobs) - VEC_TAIL else KINDS[i % 2][c]
                     left.append(pair_main(i, c, b0, nb, outs[i], cts[i], kind))
                 if k >= LAG:
                     i, b0, nb, c = jobs[k - LAG]

@@ -23,10 +23,8 @@ HH = HD // 2
 BH = B * H
 FLOPS = 2 * B * S * DIM * E
 
-KINDS = (("G", "D", "C", "G", "G", "D", "C", "G"), ("G", "D", "C", "G", "G", "G", "C", "G"))
-LAG = 4
-CT_AHEAD = 2
-CT_AT = 2
+KINDS = ("Z", "N", "Z", "N", "Z", "N", "Z", "N")
+LAG = 5
 VEC_TAIL = 2
 
 
@@ -34,7 +32,6 @@ def tile_attention_pa_kernel(tc, query_words, query_scales, wq_words, wq_scales,
     nc = tc.nc
     with ExitStack() as ctx:
         keep = ctx.enter_context(tc.tile_pool(name="keep", bufs=1))
-        ctp = ctx.enter_context(tc.tile_pool(name="ctp", bufs=CT_AHEAD + 1))
         psum = ctx.enter_context(tc.psum_pool(name="psum", bufs=6))
         psc = ctx.enter_context(tc.psum_pool(name="psc", bufs=2))
 
@@ -54,24 +51,24 @@ def tile_attention_pa_kernel(tc, query_words, query_scales, wq_words, wq_scales,
         brow = keep.tile([P, 2, P], BF16)
         bk = keep.tile([P, 2, H], BF16)
 
-        def ctab(i):
-            ct = ctp.tile([P, HD, H], F32, name="ct")
+        warm = keep.tile([P, 2], F32)
+
+        def rotated_bias(i, m):
+            rb = psc.tile([P, 2, 2 * DB, H], F32, name="cps")
             for u in range(2):
-                for v in range(2):
-                    cp = psc.tile([P, 32, H], F32, name="cps")
-                    nc.tensor.matmul(
-                        out=cp[:].rearrange("p d h -> p (d h)"), lhsT=lt[:, i, u, :],
-                        rhs=rr[:, u, 32 * v : 32 * v + 32, :].rearrange("p d h -> p (d h)"), start=True, stop=True,
-                    )
-                    d0 = HH * u + 32 * v
-                    nc.scalar.copy(out=ct[:, d0 : d0 + 32, :], in_=cp[:])
-            return ct
+                nc.tensor.matmul(
+                    out=rb[:, u].rearrange("p d h -> p (d h)"), lhsT=lt[:, i, u, :],
+                    rhs=rr[:, u, 2 * DB * m : 2 * DB * (m + 1), :].rearrange("p d h -> p (d h)"), start=True, stop=True,
+                )
+            return rb
 
         with tc.tile_pool(name="stage", bufs=1) as stage:
             wc = stage.tile([P, PASSES, 2 * E], U8, align_bytes=64)
             ws = stage.tile([P, PASSES, E], U8, align_bytes=64)
 
             nc.vector.memset(brow[:, 0, :], 0.0)
+            nc.vector.memset(warm[:, 0:1], 0.0)
+            nc.scalar.activation(out=warm[:, 1:2], in_=warm[:, 0:1], func=ACT.Copy, scale=1.0)
             nc.gpsimd.dma_start(out=cs[:], in_=cos.rearrange("a b (i p) d -> p (a b i) d", p=P))
             nc.gpsimd.dma_start(out=sn[:], in_=sin.rearrange("a b (i p) d -> p (a b i) d", p=P))
             nc.gpsimd.dma_start(out=brow[0:H, 0, :], in_=bq.rearrange("(h d) -> h d", h=H))
@@ -124,8 +121,6 @@ def tile_attention_pa_kernel(tc, query_words, query_scales, wq_words, wq_scales,
             nc.vector.tensor_copy(out=cf[:], in_=cs[:])
             nc.vector.tensor_copy(out=sg[:].rearrange("p i (u d) -> p i u d", u=2), in_=csall[:, :, :, 1, :])
 
-            cts = [ctab(i) for i in range(CT_AHEAD)]
-
             wc_v = wc[:].bitcast(I32).rearrange("p g (h c w) -> p g c h w", h=H, c=NBLK)
             wp_v = wp[:].bitcast(I32).rearrange("p g (c h w) -> p g c h w", c=NBLK, h=H)
             ws_v = ws[:].bitcast(I32).rearrange("p g (h c w) -> p g c h w", h=H, c=NBLK)
@@ -152,64 +147,61 @@ def tile_attention_pa_kernel(tc, query_words, query_scales, wq_words, wq_scales,
                         stop=(g == PASSES - 1),
                     )
 
-        def o_quad(o, n0, nn, c, s, u):
-            d0 = DB * (c + HALF * s) + 4 * u
-            return o[:, n0 : n0 + nn, d0 : d0 + 4].rearrange("p (a l) e -> p a l e", l=4)
-
-        def t_quad(t, s, u):
-            return t[:, s, 4 * u : 4 * u + 4].rearrange("p e b h -> p e (b h)").rearrange("p e (a l) -> p a l e", l=4)
-
-        def pair_main(i, c, b0, nb, o, ct, kind):
+        def banks(nb):
             if nb == B:
                 acc_lo = psum.tile([P, nb, H, DB], F32, name="acc")
                 acc_hi = psum.tile([P, nb, H, DB], F32, name="acc")
-                accs = (acc_lo[:], acc_hi[:])
-            else:
-                acc2 = psum.tile([P, 2, nb, H, DB], F32, name="acc")
-                accs = (acc2[:, 0], acc2[:, 1])
-            for s in range(2):
-                fill(accs[s], i, c + HALF * s, b0, nb)
-            if c == CT_AT and b0 == 0 and i + CT_AHEAD < NT:
-                cts.append(ctab(i + CT_AHEAD))
-            x = work.tile([P, 2, DB, nb, H], F32, name="x", bufs=5)
-            y = work.tile([P, 2, DB, nb, H], F32, name="y", bufs=7)
-            n0, nn = H * b0, H * nb
-            chain = kind == "C"
-            for s in range(2):
-                for e in range(DB):
-                    d = DB * (c + HALF * s) + e
-                    if chain:
-                        nc.vector.scalar_tensor_tensor(
-                            out=x[:, s, e], in0=accs[s][:, :, :, e], scalar=cf[:, i, d : d + 1],
-                            in1=ct[:, d, :].unsqueeze(1).to_broadcast([P, nb, H]), op0=ALU.mult, op1=ALU.add,
-                        )
-                    else:
-                        nc.scalar.activation(out=x[:, s, e], in_=accs[s][:, :, :, e], func=ACT.Copy, scale=cf[:, i, d : d + 1])
-            for t in range(2):
-                s = 1 - t
-                for e in range(DB):
-                    d = DB * (c + HALF * s) + e
-                    nc.vector.scalar_tensor_tensor(
-                        out=y[:, s, e], in0=accs[t][:, :, :, e], scalar=sg[:, i, d : d + 1],
-                        in1=(x[:, s, e] if chain else ct[:, d, :].unsqueeze(1).to_broadcast([P, nb, H])),
-                        op0=ALU.mult, op1=ALU.add,
-                    )
-            if chain:
-                return y
-            if kind == "G":
-                flat = "p s e b h -> p (s e b h)"
-                nc.gpsimd.tensor_tensor(out=y[:].rearrange(flat), in0=x[:].rearrange(flat), in1=y[:].rearrange(flat), op=ALU.add)
-                return y
-            eng = nc.vector if kind == "V" else nc.gpsimd
-            for s in range(2):
-                for u in range(2):
-                    eng.tensor_tensor(out=o_quad(o, n0, nn, c, s, u), in0=t_quad(x, s, u), in1=t_quad(y, s, u), op=ALU.add)
-            return None
+                return (acc_lo[:], acc_hi[:])
+            acc2 = psum.tile([P, 2, nb, H, DB], F32, name="acc")
+            return (acc2[:, 0], acc2[:, 1])
 
-        def unpermute(o, t, c, b0, nb):
+        def products(i, c, nb, accs, kind, xf, yf):
+            if kind == "Z":
+                x = xf.rearrange("p (s e h b) -> p s e h b", s=2, e=DB, h=H)
+                y = yf.rearrange("p (s e h b) -> p s e h b", s=2, e=DB, h=H)
+                for t in range(2):
+                    for s, dst, tab in ((t, x, cf), (1 - t, y, sg)):
+                        for e in range(DB):
+                            d = DB * (c + HALF * s) + e
+                            nc.scalar.activation(
+                                out=dst[:, s, e], in_=accs[t][:, :, :, e].rearrange("p b h -> p h b"), func=ACT.Copy,
+                                scale=tab[:, i, d : d + 1],
+                            )
+            else:
+                x = xf.rearrange("p (s n e) -> p s n e", s=2, e=DB)
+                y = yf.rearrange("p (s n e) -> p s n e", s=2, e=DB)
+                for t in range(2):
+                    for s, dst, tab in ((t, x, cf), (1 - t, y, sg)):
+                        d0 = DB * (c + HALF * s)
+                        nc.vector.tensor_tensor(
+                            out=dst[:, s], in0=accs[t].rearrange("p b h e -> p (b h) e"),
+                            in1=tab[:, i, d0 : d0 + DB].unsqueeze(1).to_broadcast([P, nb * H, DB]), op=ALU.mult,
+                        )
+
+        def finish(o, yf, rb, c, b0, nb, kind):
+            if kind == "Z":
+                y = yf.rearrange("p (s e h b) -> p s e h b", s=2, e=DB, h=H)
+            else:
+                y = yf.rearrange("p (s b h e) -> p s b h e", s=2, h=H, e=DB)
+            rows = o[:, H * b0 : H * (b0 + nb), :]
+            e0 = DB * (c % 2)
             for s in range(2):
-                for u in range(2):
-                    nc.scalar.copy(out=o_quad(o, H * b0, H * nb, c, s, u), in_=t_quad(t, s, u))
+                d0 = DB * (c + HALF * s)
+                if kind == "Z":
+                    for u in range(2):
+                        nc.vector.tensor_tensor(
+                            out=rows[:, :, d0 + 4 * u : d0 + 4 * u + 4].rearrange("p (b h) e -> p h b e", h=H),
+                            in0=y[:, s, 4 * u : 4 * u + 4].rearrange("p e h b -> p h b e"),
+                            in1=rb[:, s, e0 + 4 * u : e0 + 4 * u + 4, :].rearrange("p e h -> p h e").unsqueeze(2).to_broadcast([P, H, nb, 4]),
+                            op=ALU.add,
+                        )
+                else:
+                    nc.vector.tensor_tensor(
+                        out=rows[:, :, d0 : d0 + DB].rearrange("p (b h) e -> p b h e", h=H),
+                        in0=y[:, s],
+                        in1=rb[:, s, e0 : e0 + DB, :].rearrange("p e h -> p h e").unsqueeze(1).to_broadcast([P, nb, H, DB]),
+                        op=ALU.add,
+                    )
 
         def store(o, i, b):
             nc.sync.dma_start(
@@ -222,21 +214,36 @@ def tile_attention_pa_kernel(tc, query_words, query_scales, wq_words, wq_scales,
             for b0 in range(0, B, nb):
                 for c in range(HALF):
                     jobs.append((i, b0, nb, c))
+        n_jobs = len(jobs)
         outs = {}
-        left = []
+        sums = []
+        rbs = {}
         with tc.manual_schedule():
-            for k in range(len(jobs) + LAG):
-                if k < len(jobs):
+            for k in range(n_jobs + LAG):
+                if k < n_jobs:
                     i, b0, nb, c = jobs[k]
-                    if (b0, c) == (0, 0):
-                        o_new = opool.tile([P, BH, HD], F32, name="o")
-                        outs[i] = o_new
-                    kind = "V" if k >= len(jobs) - VEC_TAIL else KINDS[i % 2][c]
-                    left.append(pair_main(i, c, b0, nb, outs[i], cts[i], kind))
+                    accs = banks(nb)
+                    for s in range(2):
+                        fill(accs[s], i, c + HALF * s, b0, nb)
+                r = k - (LAG - 1)
+                if 0 <= r < n_jobs and jobs[r][3] % 2 == 0:
+                    rbs[r // 2] = rotated_bias(jobs[r][0], jobs[r][3] // 2)
                 if k >= LAG:
-                    i, b0, nb, c = jobs[k - LAG]
-                    if left[k - LAG] is not None:
-                        unpermute(outs[i], left[k - LAG], c, b0, nb)
-                    if c == HALF - 1:
-                        for b in range(b0, b0 + nb):
-                            store(outs[i], i, b)
+                    fi, fb0, fnb, fc = jobs[k - LAG]
+                    if (fb0, fc) == (0, 0):
+                        o_new = opool.tile([P, BH, HD], F32, name="o")
+                        outs[fi] = o_new
+                    finish(outs[fi], sums[k - LAG], rbs[(k - LAG) // 2], fc, fb0, fnb, KINDS[fc])
+                    if fc == HALF - 1:
+                        for b in range(fb0, fb0 + fnb):
+                            store(outs[fi], fi, b)
+                if k < n_jobs:
+                    if k % 2 == 0:
+                        x2 = work.tile([P, 2, 2 * DB * H * nb], F32, name="x", bufs=3)
+                        y2 = work.tile([P, 2, 2 * DB * H * nb], F32, name="y", bufs=LAG // 2 + 2)
+                    products(i, c, nb, accs, KINDS[c], x2[:, k % 2], y2[:, k % 2])
+                    sums.append(y2[:, k % 2])
+                    if k % 2 == 1:
+                        eng = nc.vector if k >= n_jobs - VEC_TAIL else nc.gpsimd
+                        flat = "p j n -> p (j n)"
+                        eng.tensor_tensor(out=y2[:].rearrange(flat), in0=x2[:].rearrange(flat), in1=y2[:].rearrange(flat), op=ALU.add)

@@ -26,6 +26,7 @@ FLOPS = 2 * B * S * DIM * E
 KINDS = ("Z", "N", "Z", "N", "Z", "N", "Z", "N")
 LAG = 5
 VEC_TAIL = 2
+X_GROUPS = ((0, 1), (1, 1), (2, 2), (4, 4))
 
 
 def tile_attention_pa_kernel(tc, query_words, query_scales, wq_words, wq_scales, bq, cos, sin, out):
@@ -35,10 +36,7 @@ def tile_attention_pa_kernel(tc, query_words, query_scales, wq_words, wq_scales,
         psum = ctx.enter_context(tc.psum_pool(name="psum", bufs=6))
         psc = ctx.enter_context(tc.psum_pool(name="psc", bufs=2))
 
-        xc = keep.tile([P, PASSES, 2 * B * S], U8, align_bytes=64)
         xs = keep.tile([P, PASSES, B * S], U8, align_bytes=64)
-        wp = keep.tile([P, PASSES, 2 * E], U8, align_bytes=64)
-        wsp = keep.tile([P, PASSES, E], U8, align_bytes=64)
         cs = keep.tile([P, NT, HD], BF16)
         sn = keep.tile([P, NT, HD], BF16)
         csall = keep.tile([P, NT, 2, 2, HH], BF16)
@@ -50,8 +48,20 @@ def tile_attention_pa_kernel(tc, query_words, query_scales, wq_words, wq_scales,
         mask = keep.tile([P, HH], BF16)
         brow = keep.tile([P, 2, P], BF16)
         bk = keep.tile([P, 2, H], BF16)
-
         warm = keep.tile([P, 2], F32)
+        x_of = {}
+        x_tiles = []
+        for i0, n in X_GROUPS:
+            xc_t = keep.tile([P, PASSES, B, 2 * P * n], U8, align_bytes=64, name="xc%d" % i0)
+            x_tiles.append(xc_t)
+            for i in range(i0, i0 + n):
+                x_of[i] = (xc_t, i - i0)
+        w_c, w_s = [], []
+        for c in range(HALF):
+            w_c_t = keep.tile([P, PASSES, 2, 2 * P], U8, align_bytes=64, name="wc%d" % c)
+            w_s_t = keep.tile([P, PASSES, 2, P], U8, align_bytes=64, name="ws%d" % c)
+            w_c.append(w_c_t)
+            w_s.append(w_s_t)
 
         def rotated_bias(i, m):
             rb = psc.tile([P, 2, 2 * DB, H], F32, name="cps")
@@ -66,50 +76,57 @@ def tile_attention_pa_kernel(tc, query_words, query_scales, wq_words, wq_scales,
             wc = stage.tile([P, PASSES, 2 * E], U8, align_bytes=64)
             ws = stage.tile([P, PASSES, E], U8, align_bytes=64)
 
+            nc.vector.memset(ws[:].bitcast(I32), 0)
+            nc.vector.memset(xs[:].bitcast(I32), 0)
             nc.vector.memset(brow[:, 0, :], 0.0)
             nc.vector.memset(warm[:, 0:1], 0.0)
             nc.scalar.activation(out=warm[:, 1:2], in_=warm[:, 0:1], func=ACT.Copy, scale=1.0)
             nc.gpsimd.dma_start(out=cs[:], in_=cos.rearrange("a b (i p) d -> p (a b i) d", p=P))
             nc.gpsimd.dma_start(out=sn[:], in_=sin.rearrange("a b (i p) d -> p (a b i) d", p=P))
             nc.gpsimd.dma_start(out=brow[0:H, 0, :], in_=bq.rearrange("(h d) -> h d", h=H))
-            nc.vector.memset(ws[:].bitcast(I32), 0)
-            nc.vector.memset(xs[:].bitcast(I32), 0)
-            for g0 in range(0, PASSES, 2):
-                nc.sync.dma_start(
-                    out=wc[:, g0 : g0 + 2, :].bitcast(I32), in_=wq_words[g0 : g0 + 2].rearrange("g p n -> p g n").bitcast(I32)
-                )
-            for q in range(4):
-                nc.sync.dma_start(
-                    out=ws[32 * q : 32 * q + 4, :, :].bitcast(I32),
-                    in_=wq_scales[:, 4 * q : 4 * q + 4, :].rearrange("g r n -> r g n").bitcast(I32),
-                )
-            xc_v = xc[:].rearrange("p g (b w) -> p g b w", b=B)
             qw_v = query_words.rearrange("g p (b w) -> g p b w", b=B)
-            for g in range(PASSES):
-                nc.sync.dma_start(out=xc_v[:, g, :, 0:256].bitcast(I32), in_=qw_v[g, :, :, 0:256].bitcast(I32))
-            for q in range(4):
+
+            def load_x(k):
+                i0, n = X_GROUPS[k]
+                for g in range(PASSES):
+                    nc.sync.dma_start(
+                        out=x_tiles[k][:, g].bitcast(I32), in_=qw_v[g, :, :, 2 * P * i0 : 2 * P * (i0 + n)].bitcast(I32)
+                    )
+
+            def load_scales(plane, rows, q):
                 nc.sync.dma_start(
-                    out=xs[32 * q : 32 * q + 4, :, :].bitcast(I32),
-                    in_=query_scales[:, 4 * q : 4 * q + 4, :].rearrange("g r n -> r g n").bitcast(I32),
+                    out=plane[32 * q : 32 * q + 4, :, :].bitcast(I32),
+                    in_=rows[:, 4 * q : 4 * q + 4, :].rearrange("g r n -> r g n").bitcast(I32),
                 )
-            for g in range(PASSES):
-                nc.sync.dma_start(out=xc_v[:, g, :, 256:2048].bitcast(I32), in_=qw_v[g, :, :, 256:2048].bitcast(I32))
+
+            with tc.manual_schedule(engines={mybir.EngineType.SP}):
+                load_x(0)
+                load_scales(ws, wq_scales, 0)
+                nc.sync.dma_start(out=wc[:].bitcast(I32), in_=wq_words.rearrange("g p n -> p g n").bitcast(I32))
+                for q in range(1, 4):
+                    load_scales(ws, wq_scales, q)
+                for q in range(4):
+                    load_scales(xs, query_scales, q)
+                for k in range(1, len(X_GROUPS)):
+                    load_x(k)
 
             make_identity(nc, ident[:])
             nc.vector.tensor_tensor(out=mask[:], in0=ident[:, 0:HH], in1=ident[:, HH:P], op=ALU.add)
             cs_v = cs[:].rearrange("p i (u d) -> p i u d", u=2)
             sn_v = sn[:].rearrange("p i (u d) -> p i u d", u=2)
-            nc.vector.tensor_copy(out=csall[:, :, :, 0, :], in_=cs_v)
-            nc.vector.tensor_scalar(out=csall[:, :, 0, 1, :], in0=sn_v[:, :, 0, :], scalar1=-1.0, scalar2=None, op0=ALU.mult)
-            nc.vector.tensor_copy(out=csall[:, :, 1, 1, :], in_=sn_v[:, :, 1, :])
+            nc.scalar.copy(out=csall[:, :, :, 0, :], in_=cs_v)
+            nc.scalar.activation(out=csall[:, :, 0, 1, :], in_=sn_v[:, :, 0, :], func=ACT.Copy, scale=-1.0)
+            nc.scalar.copy(out=csall[:, :, 1, 1, :], in_=sn_v[:, :, 1, :])
+            nc.scalar.copy(out=cf[:], in_=cs[:])
+            nc.scalar.copy(out=sg[:].rearrange("p i (u d) -> p i u d", u=2), in_=csall[:, :, :, 1, :])
             nc.vector.tensor_copy(out=brow[:, 1, 0:HH], in_=brow[:, 0, HH:HD])
             nc.vector.tensor_copy(out=brow[:, 1, HH:HD], in_=brow[:, 0, 0:HH])
             bt = psc.tile([P, 2, P], BF16, name="cps")
             for u in range(2):
                 nc.tensor.transpose(bt[:, u, :], brow[:, u, :], ident[:])
-            nc.vector.tensor_copy(out=bk[:], in_=bt[:, :, 0:H])
+            nc.scalar.copy(out=bk[:], in_=bt[:, :, 0:H])
             for u in range(2):
-                nc.vector.tensor_tensor(
+                nc.gpsimd.tensor_tensor(
                     out=rr[:, u], in0=mask[:].unsqueeze(2).to_broadcast([P, HH, H]),
                     in1=bk[:, u, :].unsqueeze(1).to_broadcast([P, HH, H]), op=ALU.mult,
                 )
@@ -117,32 +134,30 @@ def tile_attention_pa_kernel(tc, query_words, query_scales, wq_words, wq_scales,
                 tp = psc.tile([P, 4, P], BF16, name="cps")
                 for j in range(4):
                     nc.tensor.transpose(tp[:, j, :], csall[:, i0 + j // 2, j % 2].rearrange("p k d -> p (k d)"), ident[:])
-                nc.vector.tensor_copy(out=lt[:, i0 : i0 + 2].rearrange("p i u t -> p (i u) t"), in_=tp[:])
-            nc.vector.tensor_copy(out=cf[:], in_=cs[:])
-            nc.vector.tensor_copy(out=sg[:].rearrange("p i (u d) -> p i u d", u=2), in_=csall[:, :, :, 1, :])
+                nc.scalar.copy(out=lt[:, i0 : i0 + 2].rearrange("p i u t -> p (i u) t"), in_=tp[:])
 
-            wc_v = wc[:].bitcast(I32).rearrange("p g (h c w) -> p g c h w", h=H, c=NBLK)
-            wp_v = wp[:].bitcast(I32).rearrange("p g (c h w) -> p g c h w", c=NBLK, h=H)
-            ws_v = ws[:].bitcast(I32).rearrange("p g (h c w) -> p g c h w", h=H, c=NBLK)
-            wsp_v = wsp[:].bitcast(I32).rearrange("p g (c h w) -> p g c h w", c=NBLK, h=H)
-            for c0 in range(HALF):
-                for c in (c0, c0 + HALF):
-                    nc.vector.tensor_copy(out=wsp_v[:, :, c], in_=ws_v[:, :, c])
-                    nc.vector.tensor_copy(out=wp_v[:, :, c], in_=wc_v[:, :, c])
+            for c in range(HALF):
+                for src, dst, w in ((ws, w_s, 2), (wc, w_c, 4)):
+                    for s in range(2):
+                        nc.vector.tensor_copy(
+                            out=dst[c][:, :, s, :].bitcast(I32).rearrange("p g (h w) -> p g h w", h=H),
+                            in_=src[:].bitcast(I32).rearrange("p g (h s c w) -> p g s c h w", h=H, s=2, w=w)[:, :, s, c],
+                        )
 
         opool = ctx.enter_context(tc.tile_pool(name="opool", bufs=2))
         work = ctx.enter_context(tc.tile_pool(name="work", bufs=4))
 
-        def fill(view, i, c, b0, nb):
+        def fill(view, i, c, s, b0, nb):
+            xc_t, li = x_of[i]
             for j in range(nb):
                 t0 = (b0 + j) * S + i * P
                 for g in range(PASSES):
                     nc.tensor.matmul_mx(
                         out=view[:, j].rearrange("p h e -> p (h e)"),
-                        lhsT=xc[:, g, 2 * t0 : 2 * t0 + 256].bitcast(FP4),
+                        lhsT=xc_t[:, g, b0 + j, 2 * P * li : 2 * P * (li + 1)].bitcast(FP4),
                         lhsT_scale=xs[:, g, t0 : t0 + P],
-                        rhs=wp[:, g, 256 * c : 256 * c + 256].bitcast(FP4),
-                        rhs_scale=wsp[:, g, P * c : P * c + P],
+                        rhs=w_c[c][:, g, s, :].bitcast(FP4),
+                        rhs_scale=w_s[c][:, g, s, :],
                         start=(g == 0),
                         stop=(g == PASSES - 1),
                     )
@@ -224,7 +239,7 @@ def tile_attention_pa_kernel(tc, query_words, query_scales, wq_words, wq_scales,
                     i, b0, nb, c = jobs[k]
                     accs = banks(nb)
                     for s in range(2):
-                        fill(accs[s], i, c + HALF * s, b0, nb)
+                        fill(accs[s], i, c, s, b0, nb)
                 r = k - (LAG - 1)
                 if 0 <= r < n_jobs and jobs[r][3] % 2 == 0:
                     rbs[r // 2] = rotated_bias(jobs[r][0], jobs[r][3] // 2)

@@ -63,6 +63,23 @@ def tile_attention_pa_kernel(tc, query_words, query_scales, wq_words, wq_scales,
             w_c.append(w_c_t)
             w_s.append(w_s_t)
 
+        def bias_table():
+            bt = psc.tile([P, 2, P], BF16, name="cps")
+            for u in range(2):
+                nc.tensor.transpose(bt[:, u, :], brow[:, u, :], ident[:])
+            nc.scalar.copy(out=bk[:], in_=bt[:, :, 0:H])
+            for u in range(2):
+                nc.gpsimd.tensor_tensor(
+                    out=rr[:, u], in0=mask[:].unsqueeze(2).to_broadcast([P, HH, H]),
+                    in1=bk[:, u, :].unsqueeze(1).to_broadcast([P, HH, H]), op=ALU.mult,
+                )
+
+        def turn_tables(i0):
+            tp = psc.tile([P, 4, P], BF16, name="cps")
+            for j in range(4):
+                nc.tensor.transpose(tp[:, j, :], csall[:, i0 + j // 2, j % 2].rearrange("p k d -> p (k d)"), ident[:])
+            nc.scalar.copy(out=lt[:, i0 : i0 + 2].rearrange("p i u t -> p (i u) t"), in_=tp[:])
+
         def rotated_bias(i, m):
             rb = psc.tile([P, 2, 2 * DB, H], F32, name="cps")
             for u in range(2):
@@ -76,10 +93,10 @@ def tile_attention_pa_kernel(tc, query_words, query_scales, wq_words, wq_scales,
             wc = stage.tile([P, PASSES, 2 * E], U8, align_bytes=64)
             ws = stage.tile([P, PASSES, E], U8, align_bytes=64)
 
-            nc.vector.memset(ws[:].bitcast(I32), 0)
-            nc.vector.memset(xs[:].bitcast(I32), 0)
             nc.vector.memset(brow[:, 0, :], 0.0)
             nc.vector.memset(warm[:, 0:1], 0.0)
+            nc.vector.memset(ws[:].bitcast(I32), 0)
+            nc.vector.memset(xs[:].bitcast(I32), 0)
             nc.scalar.activation(out=warm[:, 1:2], in_=warm[:, 0:1], func=ACT.Copy, scale=1.0)
             nc.gpsimd.dma_start(out=cs[:], in_=cos.rearrange("a b (i p) d -> p (a b i) d", p=P))
             nc.gpsimd.dma_start(out=sn[:], in_=sin.rearrange("a b (i p) d -> p (a b i) d", p=P))
@@ -95,8 +112,8 @@ def tile_attention_pa_kernel(tc, query_words, query_scales, wq_words, wq_scales,
 
             def load_scales(plane, rows, q):
                 nc.sync.dma_start(
-                    out=plane[32 * q : 32 * q + 4, :, :].bitcast(I32),
-                    in_=rows[:, 4 * q : 4 * q + 4, :].rearrange("g r n -> r g n").bitcast(I32),
+                    out=plane[q : P : 32, :, :].bitcast(I32),
+                    in_=rows[:, q : 16 : 4, :].rearrange("g r n -> r g n").bitcast(I32),
                 )
 
             with tc.manual_schedule(engines={mybir.EngineType.SP}):
@@ -121,20 +138,6 @@ def tile_attention_pa_kernel(tc, query_words, query_scales, wq_words, wq_scales,
             nc.scalar.copy(out=sg[:].rearrange("p i (u d) -> p i u d", u=2), in_=csall[:, :, :, 1, :])
             nc.vector.tensor_copy(out=brow[:, 1, 0:HH], in_=brow[:, 0, HH:HD])
             nc.vector.tensor_copy(out=brow[:, 1, HH:HD], in_=brow[:, 0, 0:HH])
-            bt = psc.tile([P, 2, P], BF16, name="cps")
-            for u in range(2):
-                nc.tensor.transpose(bt[:, u, :], brow[:, u, :], ident[:])
-            nc.scalar.copy(out=bk[:], in_=bt[:, :, 0:H])
-            for u in range(2):
-                nc.gpsimd.tensor_tensor(
-                    out=rr[:, u], in0=mask[:].unsqueeze(2).to_broadcast([P, HH, H]),
-                    in1=bk[:, u, :].unsqueeze(1).to_broadcast([P, HH, H]), op=ALU.mult,
-                )
-            for i0 in range(0, NT, 2):
-                tp = psc.tile([P, 4, P], BF16, name="cps")
-                for j in range(4):
-                    nc.tensor.transpose(tp[:, j, :], csall[:, i0 + j // 2, j % 2].rearrange("p k d -> p (k d)"), ident[:])
-                nc.scalar.copy(out=lt[:, i0 : i0 + 2].rearrange("p i u t -> p (i u) t"), in_=tp[:])
 
             for c in range(HALF):
                 for src, dst, w in ((ws, w_s, 2), (wc, w_c, 4)):
@@ -240,6 +243,10 @@ def tile_attention_pa_kernel(tc, query_words, query_scales, wq_words, wq_scales,
                     accs = banks(nb)
                     for s in range(2):
                         fill(accs[s], i, c, s, b0, nb)
+                if k == 0:
+                    bias_table()
+                if 2 * k < NT:
+                    turn_tables(2 * k)
                 r = k - (LAG - 1)
                 if 0 <= r < n_jobs and jobs[r][3] % 2 == 0:
                     rbs[r // 2] = rotated_bias(jobs[r][0], jobs[r][3] // 2)

@@ -23,9 +23,9 @@ HH = HD // 2
 BH = B * H
 FLOPS = 2 * B * S * DIM * E
 
-KINDS = ("Z", "N", "Z", "N", "Z", "N", "Z", "N")
+KINDS = ("Z", "N", "Z", "Z", "N", "Z", "Y", "Z")
+LAST_KINDS = ("Z", "N", "Z", "N", "Z", "N", "Z", "N")
 LAG = 5
-VEC_TAIL = 2
 X_GROUPS = ((0, 1), (1, 1), (2, 2), (4, 4))
 
 
@@ -75,7 +75,7 @@ def tile_attention_pa_kernel(tc, query_words, query_scales, wq_words, wq_scales,
                 )
 
         def turn_tables(i0):
-            tp = psc.tile([P, 4, P], BF16, name="cps")
+            tp = psum.tile([P, 4, P], BF16, name="acc")
             for j in range(4):
                 nc.tensor.transpose(tp[:, j, :], csall[:, i0 + j // 2, j % 2].rearrange("p k d -> p (k d)"), ident[:])
             nc.scalar.copy(out=lt[:, i0 : i0 + 2].rearrange("p i u t -> p (i u) t"), in_=tp[:])
@@ -98,9 +98,9 @@ def tile_attention_pa_kernel(tc, query_words, query_scales, wq_words, wq_scales,
             nc.vector.memset(ws[:].bitcast(I32), 0)
             nc.vector.memset(xs[:].bitcast(I32), 0)
             nc.scalar.activation(out=warm[:, 1:2], in_=warm[:, 0:1], func=ACT.Copy, scale=1.0)
-            nc.gpsimd.dma_start(out=cs[:], in_=cos.rearrange("a b (i p) d -> p (a b i) d", p=P))
-            nc.gpsimd.dma_start(out=sn[:], in_=sin.rearrange("a b (i p) d -> p (a b i) d", p=P))
-            nc.gpsimd.dma_start(out=brow[0:H, 0, :], in_=bq.rearrange("(h d) -> h d", h=H))
+            nc.scalar.dma_start(out=cs[:], in_=cos.rearrange("a b (i p) d -> p (a b i) d", p=P))
+            nc.scalar.dma_start(out=sn[:], in_=sin.rearrange("a b (i p) d -> p (a b i) d", p=P))
+            nc.scalar.dma_start(out=brow[0:H, 0, :], in_=bq.rearrange("(h d) -> h d", h=H))
             qw_v = query_words.rearrange("g p (b w) -> g p b w", b=B)
 
             def load_x(k):
@@ -131,13 +131,19 @@ def tile_attention_pa_kernel(tc, query_words, query_scales, wq_words, wq_scales,
             nc.vector.tensor_tensor(out=mask[:], in0=ident[:, 0:HH], in1=ident[:, HH:P], op=ALU.add)
             cs_v = cs[:].rearrange("p i (u d) -> p i u d", u=2)
             sn_v = sn[:].rearrange("p i (u d) -> p i u d", u=2)
+            sg_v = sg[:].rearrange("p i (u d) -> p i u d", u=2)
             nc.scalar.copy(out=csall[:, :, :, 0, :], in_=cs_v)
             nc.scalar.activation(out=csall[:, :, 0, 1, :], in_=sn_v[:, :, 0, :], func=ACT.Copy, scale=-1.0)
             nc.scalar.copy(out=csall[:, :, 1, 1, :], in_=sn_v[:, :, 1, :])
-            nc.scalar.copy(out=cf[:], in_=cs[:])
-            nc.scalar.copy(out=sg[:].rearrange("p i (u d) -> p i u d", u=2), in_=csall[:, :, :, 1, :])
             nc.vector.tensor_copy(out=brow[:, 1, 0:HH], in_=brow[:, 0, HH:HD])
             nc.vector.tensor_copy(out=brow[:, 1, HH:HD], in_=brow[:, 0, 0:HH])
+            bias_table()
+            for i0 in range(0, NT, 2):
+                turn_tables(i0)
+            for tiles in (slice(0, 1), slice(1, NT)):
+                nc.scalar.copy(out=cf[:, tiles], in_=cs[:, tiles])
+                nc.scalar.activation(out=sg_v[:, tiles, 0, :], in_=sn_v[:, tiles, 0, :], func=ACT.Copy, scale=-1.0)
+                nc.scalar.copy(out=sg_v[:, tiles, 1, :], in_=sn_v[:, tiles, 1, :])
 
             for c in range(HALF):
                 for src, dst, w in ((ws, w_s, 2), (wc, w_c, 4)):
@@ -174,7 +180,24 @@ def tile_attention_pa_kernel(tc, query_words, query_scales, wq_words, wq_scales,
             return (acc2[:, 0], acc2[:, 1])
 
         def products(i, c, nb, accs, kind, xf, yf):
-            if kind == "Z":
+            if kind == "Y":
+                x = xf.rearrange("p (s e h b) -> p s e h b", s=2, e=DB, h=H)
+                y = yf.rearrange("p (s e h b) -> p s e h b", s=2, e=DB, h=H)
+                for s in range(2):
+                    for e in range(DB):
+                        d = DB * (c + HALF * s) + e
+                        nc.scalar.activation(
+                            out=x[:, s, e], in_=accs[s][:, :, :, e].rearrange("p b h -> p h b"), func=ACT.Copy,
+                            scale=cf[:, i, d : d + 1],
+                        )
+                for s in range(2):
+                    for e in range(DB):
+                        d = DB * (c + HALF * s) + e
+                        nc.vector.scalar_tensor_tensor(
+                            out=y[:, s, e], in0=accs[1 - s][:, :, :, e].rearrange("p b h -> p h b"), scalar=sg[:, i, d : d + 1],
+                            in1=x[:, s, e], op0=ALU.mult, op1=ALU.add,
+                        )
+            elif kind == "Z":
                 x = xf.rearrange("p (s e h b) -> p s e h b", s=2, e=DB, h=H)
                 y = yf.rearrange("p (s e h b) -> p s e h b", s=2, e=DB, h=H)
                 for t in range(2):
@@ -197,7 +220,7 @@ def tile_attention_pa_kernel(tc, query_words, query_scales, wq_words, wq_scales,
                         )
 
         def finish(o, yf, rb, c, b0, nb, kind):
-            if kind == "Z":
+            if kind != "N":
                 y = yf.rearrange("p (s e h b) -> p s e h b", s=2, e=DB, h=H)
             else:
                 y = yf.rearrange("p (s b h e) -> p s b h e", s=2, h=H, e=DB)
@@ -205,7 +228,7 @@ def tile_attention_pa_kernel(tc, query_words, query_scales, wq_words, wq_scales,
             e0 = DB * (c % 2)
             for s in range(2):
                 d0 = DB * (c + HALF * s)
-                if kind == "Z":
+                if kind != "N":
                     for u in range(2):
                         nc.vector.tensor_tensor(
                             out=rows[:, :, d0 + 4 * u : d0 + 4 * u + 4].rearrange("p (b h) e -> p h b e", h=H),
@@ -236,6 +259,11 @@ def tile_attention_pa_kernel(tc, query_words, query_scales, wq_words, wq_scales,
         outs = {}
         sums = []
         rbs = {}
+        place = 0
+
+        def kinds_of(i):
+            return LAST_KINDS if i == NT - 1 else KINDS
+
         with tc.manual_schedule():
             for k in range(n_jobs + LAG):
                 if k < n_jobs:
@@ -243,10 +271,6 @@ def tile_attention_pa_kernel(tc, query_words, query_scales, wq_words, wq_scales,
                     accs = banks(nb)
                     for s in range(2):
                         fill(accs[s], i, c, s, b0, nb)
-                if k == 0:
-                    bias_table()
-                if 2 * k < NT:
-                    turn_tables(2 * k)
                 r = k - (LAG - 1)
                 if 0 <= r < n_jobs and jobs[r][3] % 2 == 0:
                     rbs[r // 2] = rotated_bias(jobs[r][0], jobs[r][3] // 2)
@@ -255,17 +279,32 @@ def tile_attention_pa_kernel(tc, query_words, query_scales, wq_words, wq_scales,
                     if (fb0, fc) == (0, 0):
                         o_new = opool.tile([P, BH, HD], F32, name="o")
                         outs[fi] = o_new
-                    finish(outs[fi], sums[k - LAG], rbs[(k - LAG) // 2], fc, fb0, fnb, KINDS[fc])
+                    finish(outs[fi], sums[k - LAG], rbs[(k - LAG) // 2], fc, fb0, fnb, kinds_of(fi)[fc])
                     if fc == HALF - 1:
                         for b in range(fb0, fb0 + fnb):
                             store(outs[fi], fi, b)
                 if k < n_jobs:
-                    if k % 2 == 0:
-                        x2 = work.tile([P, 2, 2 * DB * H * nb], F32, name="x", bufs=3)
-                        y2 = work.tile([P, 2, 2 * DB * H * nb], F32, name="y", bufs=LAG // 2 + 2)
-                    products(i, c, nb, accs, KINDS[c], x2[:, k % 2], y2[:, k % 2])
-                    sums.append(y2[:, k % 2])
-                    if k % 2 == 1:
-                        eng = nc.vector if k >= n_jobs - VEC_TAIL else nc.gpsimd
-                        flat = "p j n -> p (j n)"
-                        eng.tensor_tensor(out=y2[:].rearrange(flat), in0=x2[:].rearrange(flat), in1=y2[:].rearrange(flat), op=ALU.add)
+                    size = 2 * DB * H * nb
+                    kind = kinds_of(i)[c]
+                    last_c = max(cc for cc in range(HALF) if kinds_of(i)[cc] != "Y")
+                    if kind == "Y":
+                        x1 = work.tile([P, size], F32, name="xy", bufs=1)
+                        y1 = work.tile([P, size], F32, name="yy", bufs=2)
+                        products(i, c, nb, accs, "Y", x1[:], y1[:])
+                        sums.append(y1[:])
+                    else:
+                        if place == 0:
+                            x2 = work.tile([P, 2, size], F32, name="x", bufs=3)
+                            y2 = work.tile([P, 2, size], F32, name="y", bufs=LAG // 2 + 2)
+                        products(i, c, nb, accs, kind, x2[:, place], y2[:, place])
+                        sums.append(y2[:, place])
+                        if place == 1 or c == last_c:
+                            eng = nc.vector if k >= n_jobs - 2 else nc.gpsimd
+                            nc_view = slice(0, place + 1)
+                            flat = "p j n -> p (j n)"
+                            eng.tensor_tensor(
+                                out=y2[:, nc_view].rearrange(flat), in0=x2[:, nc_view].rearrange(flat), in1=y2[:, nc_view].rearrange(flat), op=ALU.add
+                            )
+                            place = 0
+                        else:
+                            place = 1

@@ -27,19 +27,27 @@ KINDS = ("Z", "N", "Z", "Z", "N", "Z", "Y", "Z")
 LAST_KINDS = ("Z", "N", "Z", "N", "Z", "N", "Z", "N")
 LAG = 5
 X_GROUPS = ((0, 1), (1, 1), (2, 2), (4, 4))
+NAT = ((0, 0),)
+JOBSETS = ((0, 1, 3), (1, 0, 4), (2, 0, 4), (3, 0, 4), (4, 0, 4), (5, 0, 4), (6, 0, 4), (7, 0, 2), (7, 2, 2))
+HG = 8
+NAT_FIRST = 4
+NAT_EVERY = 1
+PERM_HEAD = 4
 
 
 def tile_attention_pa_kernel(tc, query_words, query_scales, wq_words, wq_scales, bq, cos, sin, out):
     nc = tc.nc
+    n_nat = len(NAT)
     with ExitStack() as ctx:
         keep = ctx.enter_context(tc.tile_pool(name="keep", bufs=1))
+        ovl = ctx.enter_context(tc.tile_pool(name="ovl", bufs=1))
+        opool = ctx.enter_context(tc.tile_pool(name="opool", bufs=1))
+        work = ctx.enter_context(tc.tile_pool(name="work", bufs=4))
         psum = ctx.enter_context(tc.psum_pool(name="psum", bufs=6))
         psc = ctx.enter_context(tc.psum_pool(name="psc", bufs=2))
+        ctx.enter_context(tc.manual_schedule())
 
         xs = keep.tile([P, PASSES, B * S], U8, align_bytes=64)
-        cs = keep.tile([P, NT, HD], BF16)
-        sn = keep.tile([P, NT, HD], BF16)
-        csall = keep.tile([P, NT, 2, 2, HH], BF16)
         cf = keep.tile([P, NT, HD], F32)
         sg = keep.tile([P, NT, HD], F32)
         lt = keep.tile([P, NT, 2, P], BF16)
@@ -49,6 +57,14 @@ def tile_attention_pa_kernel(tc, query_words, query_scales, wq_words, wq_scales,
         brow = keep.tile([P, 2, P], BF16)
         bk = keep.tile([P, 2, H], BF16)
         warm = keep.tile([P, 2], F32)
+        bias_bc = keep.tile([P, H, HD], BF16)
+        xn = keep.tile([P, n_nat, PASSES, 2 * P], U8, align_bytes=64)
+        xsn = keep.tile([P, n_nat, PASSES, P], U8, align_bytes=64)
+        yn = keep.tile([P, HG, HD], F32)
+        tn = []
+        for u in range(n_nat):
+            tn_t = keep.tile([P, H, HD], F32, name="tn%d" % u)
+            tn.append(tn_t)
         x_of = {}
         x_tiles = []
         for i0, n in X_GROUPS:
@@ -62,6 +78,21 @@ def tile_attention_pa_kernel(tc, query_words, query_scales, wq_words, wq_scales,
             w_s_t = keep.tile([P, PASSES, 2, P], U8, align_bytes=64, name="ws%d" % c)
             w_c.append(w_c_t)
             w_s.append(w_s_t)
+        wc = ovl.tile([P, PASSES, 2 * E], U8, align_bytes=64, offset=0)
+        ws = ovl.tile([P, PASSES, E], U8, align_bytes=64, offset=16384)
+        cs = ovl.tile([P, NT, HD], BF16, align_bytes=64, offset=24576)
+        sn = ovl.tile([P, NT, HD], BF16, align_bytes=64, offset=26624)
+        csall = ovl.tile([P, NT, 2, 2, HH], BF16, align_bytes=64, offset=28672)
+
+        def bias_rows():
+            for j in range(4):
+                bb = psum.tile([P, 4, HD], F32, name="acc")
+                for h4 in range(4):
+                    h = 4 * j + h4
+                    nc.tensor.matmul(
+                        out=bb[:, h4, :], lhsT=ident[:, h : h + 1].to_broadcast([P, P]), rhs=brow[:, 0, :], start=True, stop=True
+                    )
+                nc.scalar.copy(out=bias_bc[:, 4 * j : 4 * j + 4, :], in_=bb[:])
 
         def bias_table():
             bt = psc.tile([P, 2, P], BF16, name="cps")
@@ -74,8 +105,8 @@ def tile_attention_pa_kernel(tc, query_words, query_scales, wq_words, wq_scales,
                     in1=bk[:, u, :].unsqueeze(1).to_broadcast([P, HH, H]), op=ALU.mult,
                 )
 
-        def turn_tables(i0):
-            tp = psum.tile([P, 4, P], BF16, name="acc")
+        def turn_tables(i0, pool, tag):
+            tp = pool.tile([P, 4, P], BF16, name=tag)
             for j in range(4):
                 nc.tensor.transpose(tp[:, j, :], csall[:, i0 + j // 2, j % 2].rearrange("p k d -> p (k d)"), ident[:])
             nc.scalar.copy(out=lt[:, i0 : i0 + 2].rearrange("p i u t -> p (i u) t"), in_=tp[:])
@@ -89,72 +120,160 @@ def tile_attention_pa_kernel(tc, query_words, query_scales, wq_words, wq_scales,
                 )
             return rb
 
-        with tc.tile_pool(name="stage", bufs=1) as stage:
-            wc = stage.tile([P, PASSES, 2 * E], U8, align_bytes=64)
-            ws = stage.tile([P, PASSES, E], U8, align_bytes=64)
+        nc.vector.memset(brow[:, 0, :], 0.0)
+        nc.vector.memset(warm[:, 0:1], 0.0)
+        nc.vector.memset(xsn[:].rearrange("p u g n -> p (u g n)").bitcast(I32), 0)
+        nc.vector.memset(ws[:].bitcast(I32), 0)
+        nc.vector.memset(xs[:].bitcast(I32), 0)
+        nc.scalar.activation(out=warm[:, 1:2], in_=warm[:, 0:1], func=ACT.Copy, scale=1.0)
+        make_identity(nc, ident[:])
+        nc.gpsimd.dma_start(out=cs[:], in_=cos.rearrange("a b (i p) d -> p (a b i) d", p=P))
+        nc.gpsimd.dma_start(out=sn[:], in_=sin.rearrange("a b (i p) d -> p (a b i) d", p=P))
+        qw_v = query_words.rearrange("g p (b w) -> g p b w", b=B)
 
-            nc.vector.memset(brow[:, 0, :], 0.0)
-            nc.vector.memset(warm[:, 0:1], 0.0)
-            nc.vector.memset(ws[:].bitcast(I32), 0)
-            nc.vector.memset(xs[:].bitcast(I32), 0)
-            nc.scalar.activation(out=warm[:, 1:2], in_=warm[:, 0:1], func=ACT.Copy, scale=1.0)
-            nc.scalar.dma_start(out=cs[:], in_=cos.rearrange("a b (i p) d -> p (a b i) d", p=P))
-            nc.scalar.dma_start(out=sn[:], in_=sin.rearrange("a b (i p) d -> p (a b i) d", p=P))
-            nc.scalar.dma_start(out=brow[0:H, 0, :], in_=bq.rearrange("(h d) -> h d", h=H))
-            qw_v = query_words.rearrange("g p (b w) -> g p b w", b=B)
-
-            def load_x(k):
-                i0, n = X_GROUPS[k]
-                for g in range(PASSES):
-                    nc.sync.dma_start(
-                        out=x_tiles[k][:, g].bitcast(I32), in_=qw_v[g, :, :, 2 * P * i0 : 2 * P * (i0 + n)].bitcast(I32)
-                    )
-
-            def load_scales(plane, rows, q):
+        def load_x(k):
+            i0, n = X_GROUPS[k]
+            for g in range(PASSES):
                 nc.sync.dma_start(
-                    out=plane[q : P : 32, :, :].bitcast(I32),
-                    in_=rows[:, q : 16 : 4, :].rearrange("g r n -> r g n").bitcast(I32),
+                    out=x_tiles[k][:, g].bitcast(I32), in_=qw_v[g, :, :, 2 * P * i0 : 2 * P * (i0 + n)].bitcast(I32)
                 )
 
-            with tc.manual_schedule(engines={mybir.EngineType.SP}):
-                load_x(0)
-                load_scales(ws, wq_scales, 0)
-                nc.sync.dma_start(out=wc[:].bitcast(I32), in_=wq_words.rearrange("g p n -> p g n").bitcast(I32))
-                for q in range(1, 4):
-                    load_scales(ws, wq_scales, q)
-                for q in range(4):
-                    load_scales(xs, query_scales, q)
-                for k in range(1, len(X_GROUPS)):
-                    load_x(k)
+        def load_scales(plane, rows, q):
+            nc.sync.dma_start(
+                out=plane[q : P : 32, :, :].bitcast(I32),
+                in_=rows[:, q : 16 : 4, :].rearrange("g r n -> r g n").bitcast(I32),
+            )
 
-            make_identity(nc, ident[:])
-            nc.vector.tensor_tensor(out=mask[:], in0=ident[:, 0:HH], in1=ident[:, HH:P], op=ALU.add)
-            cs_v = cs[:].rearrange("p i (u d) -> p i u d", u=2)
-            sn_v = sn[:].rearrange("p i (u d) -> p i u d", u=2)
-            sg_v = sg[:].rearrange("p i (u d) -> p i u d", u=2)
-            nc.scalar.copy(out=csall[:, :, :, 0, :], in_=cs_v)
-            nc.scalar.activation(out=csall[:, :, 0, 1, :], in_=sn_v[:, :, 0, :], func=ACT.Copy, scale=-1.0)
-            nc.scalar.copy(out=csall[:, :, 1, 1, :], in_=sn_v[:, :, 1, :])
-            nc.vector.tensor_copy(out=brow[:, 1, 0:HH], in_=brow[:, 0, HH:HD])
-            nc.vector.tensor_copy(out=brow[:, 1, HH:HD], in_=brow[:, 0, 0:HH])
-            bias_table()
-            for i0 in range(0, NT, 2):
-                turn_tables(i0)
-            for tiles in (slice(0, 1), slice(1, NT)):
-                nc.scalar.copy(out=cf[:, tiles], in_=cs[:, tiles])
-                nc.scalar.activation(out=sg_v[:, tiles, 0, :], in_=sn_v[:, tiles, 0, :], func=ACT.Copy, scale=-1.0)
-                nc.scalar.copy(out=sg_v[:, tiles, 1, :], in_=sn_v[:, tiles, 1, :])
+        def load_nat(u):
+            t0 = NAT[u][1] * S + NAT[u][0] * P
+            nc.sync.dma_start(
+                out=xn[:, u].bitcast(I32), in_=query_words[:, :, 2 * t0 : 2 * (t0 + P)].rearrange("g p w -> p g w").bitcast(I32)
+            )
+            for q in range(4):
+                nc.sync.dma_start(
+                    out=xsn[q : P : 32, u].bitcast(I32),
+                    in_=query_scales[:, q : 16 : 4, t0 : t0 + P].rearrange("g r n -> r g n").bitcast(I32),
+                )
 
-            for c in range(HALF):
-                for src, dst, w in ((ws, w_s, 2), (wc, w_c, 4)):
-                    for s in range(2):
-                        nc.vector.tensor_copy(
-                            out=dst[c][:, :, s, :].bitcast(I32).rearrange("p g (h w) -> p g h w", h=H),
-                            in_=src[:].bitcast(I32).rearrange("p g (h s c w) -> p g s c h w", h=H, s=2, w=w)[:, :, s, c],
-                        )
+        def load_w(g):
+            nc.sync.dma_start(out=wc[:, g].bitcast(I32), in_=wq_words[g].bitcast(I32))
 
-        opool = ctx.enter_context(tc.tile_pool(name="opool", bufs=2))
-        work = ctx.enter_context(tc.tile_pool(name="work", bufs=4))
+        nc.sync.dma_start(out=brow[0:H, 0, :], in_=bq.rearrange("(h d) -> h d", h=H))
+        load_nat(0)
+        load_w(0)
+        for q in range(4):
+            load_scales(ws, wq_scales, q)
+        for g in range(1, PASSES):
+            load_w(g)
+        for u in range(1, n_nat):
+            load_nat(u)
+        for q in range(4):
+            load_scales(xs, query_scales, q)
+        for k in range(len(X_GROUPS)):
+            load_x(k)
+
+        nc.vector.tensor_tensor(out=mask[:], in0=ident[:, 0:HH], in1=ident[:, HH:P], op=ALU.add)
+        nc.vector.tensor_copy(out=brow[:, 1, 0:HH], in_=brow[:, 0, HH:HD])
+        nc.vector.tensor_copy(out=brow[:, 1, HH:HD], in_=brow[:, 0, 0:HH])
+        bias_rows()
+        bias_table()
+        cs_v = cs[:].rearrange("p i (u d) -> p i u d", u=2)
+        sn_v = sn[:].rearrange("p i (u d) -> p i u d", u=2)
+        sg_v = sg[:].rearrange("p i (u d) -> p i u d", u=2)
+        nc.scalar.copy(out=csall[:, :, :, 0, :], in_=cs_v)
+        nc.scalar.activation(out=csall[:, :, 0, 1, :], in_=sn_v[:, :, 0, :], func=ACT.Copy, scale=-1.0)
+        nc.scalar.copy(out=csall[:, :, 1, 1, :], in_=sn_v[:, :, 1, :])
+        for tiles in (slice(0, 1), slice(1, NT)):
+            nc.scalar.copy(out=cf[:, tiles], in_=cs[:, tiles])
+            nc.scalar.activation(out=sg_v[:, tiles, 0, :], in_=sn_v[:, tiles, 0, :], func=ACT.Copy, scale=-1.0)
+            nc.scalar.copy(out=sg_v[:, tiles, 1, :], in_=sn_v[:, tiles, 1, :])
+
+        def nat_pass(acc, u, j, g):
+            nc.tensor.matmul_mx(
+                out=acc[:].rearrange("p h d -> p (h d)"),
+                lhsT=xn[:, u, g, :].bitcast(FP4),
+                lhsT_scale=xsn[:, u, g, :],
+                rhs=wc[:, g, 1024 * j : 1024 * (j + 1)].bitcast(FP4),
+                rhs_scale=ws[:, g, 512 * j : 512 * (j + 1)],
+                start=(g == 0),
+                stop=(g == PASSES - 1),
+            )
+
+        nat_acc = {}
+        for u in range(n_nat):
+            for j in range(4):
+                acc_n = psum.tile([P, 4, HD], F32, name="acc")
+                nat_acc[(u, j)] = acc_n
+                if u > 0:
+                    for g in range(PASSES):
+                        nat_pass(acc_n, u, j, g)
+            if u == 0:
+                for g in range(PASSES):
+                    for j in range(4):
+                        nat_pass(nat_acc[(0, j)], 0, j, g)
+
+        turn_tables(0, psum, "acc")
+        turn_tables(2, psum, "acc")
+        turn_tables(4, psc, "cps")
+        turn_tables(6, psc, "cps")
+
+        def permute(c):
+            for src, dst, w in ((ws, w_s, 2), (wc, w_c, 4)):
+                for s in range(2):
+                    nc.vector.tensor_copy(
+                        out=dst[c][:, :, s, :].bitcast(I32).rearrange("p g (h w) -> p g h w", h=H),
+                        in_=src[:].bitcast(I32).rearrange("p g (h s c w) -> p g s c h w", h=H, s=2, w=w)[:, :, s, c],
+                    )
+
+        def nat_bias(u, j):
+            nc.vector.tensor_tensor(
+                out=tn[u][:, 4 * j : 4 * j + 4, :], in0=nat_acc[(u, j)][:], in1=bias_bc[:, 4 * j : 4 * j + 4, :], op=ALU.add
+            )
+
+        permute(0)
+        done_perm = 1
+        for u in range(n_nat):
+            for j0 in (0, 2):
+                nat_bias(u, j0)
+                nat_bias(u, j0 + 1)
+                if done_perm < PERM_HEAD:
+                    permute(done_perm)
+                    done_perm += 1
+        for c in range(done_perm, PERM_HEAD):
+            permute(c)
+        done_perm = max(done_perm, PERM_HEAD)
+
+        nat_steps = []
+        for u in range(n_nat):
+            for h0 in range(0, H, HG):
+                for part in range(4):
+                    nat_steps.append((u, h0, part))
+        state = {"nat": 0, "adds": 0}
+
+        def nat_step():
+            if state["nat"] >= len(nat_steps):
+                return
+            u, h0, part = nat_steps[state["nat"]]
+            state["nat"] += 1
+            i, b = NAT[u]
+            tv = tn[u][:, h0 : h0 + HG, :]
+            if part == 0:
+                nc.gpsimd.tensor_tensor(
+                    out=yn[:, :, 0:HH], in0=tv[:, :, HH:HD], in1=sg[:, i, 0:HH].unsqueeze(1).to_broadcast([P, HG, HH]), op=ALU.mult
+                )
+            elif part == 1:
+                nc.gpsimd.tensor_tensor(
+                    out=yn[:, :, HH:HD], in0=tv[:, :, 0:HH], in1=sg[:, i, HH:HD].unsqueeze(1).to_broadcast([P, HG, HH]), op=ALU.mult
+                )
+            elif part == 2:
+                nc.gpsimd.tensor_tensor(out=tv, in0=tv, in1=cf[:, i, :].unsqueeze(1).to_broadcast([P, HG, HD]), op=ALU.mult)
+            else:
+                nc.gpsimd.tensor_tensor(out=tv, in0=tv, in1=yn[:], op=ALU.add)
+                if h0 + HG == H:
+                    nc.sync.dma_start(out=out[b, :, P * i : P * (i + 1), :].rearrange("h p d -> p h d"), in_=tn[u][:])
+
+        for rep in range(NAT_FIRST):
+            nat_step()
 
         def fill(view, i, c, s, b0, nb):
             xc_t, li = x_of[i]
@@ -172,7 +291,7 @@ def tile_attention_pa_kernel(tc, query_words, query_scales, wq_words, wq_scales,
                     )
 
         def banks(nb):
-            if nb == B:
+            if 2 * nb * P > 512:
                 acc_lo = psum.tile([P, nb, H, DB], F32, name="acc")
                 acc_hi = psum.tile([P, nb, H, DB], F32, name="acc")
                 return (acc_lo[:], acc_hi[:])
@@ -250,61 +369,69 @@ def tile_attention_pa_kernel(tc, query_words, query_scales, wq_words, wq_scales,
             )
 
         jobs = []
-        for i in range(NT):
-            nb = B // 2 if i == NT - 1 else B
-            for b0 in range(0, B, nb):
-                for c in range(HALF):
-                    jobs.append((i, b0, nb, c))
+        for i, b0, nb in JOBSETS:
+            for c in range(HALF):
+                jobs.append((i, b0, nb, c))
         n_jobs = len(jobs)
         outs = {}
         sums = []
         rbs = {}
         place = 0
 
-        def kinds_of(i):
-            return LAST_KINDS if i == NT - 1 else KINDS
+        def kinds_of(nb):
+            return LAST_KINDS if nb <= 2 else KINDS
 
-        with tc.manual_schedule():
-            for k in range(n_jobs + LAG):
-                if k < n_jobs:
-                    i, b0, nb, c = jobs[k]
-                    accs = banks(nb)
-                    for s in range(2):
-                        fill(accs[s], i, c, s, b0, nb)
-                r = k - (LAG - 1)
-                if 0 <= r < n_jobs and jobs[r][3] % 2 == 0:
-                    rbs[r // 2] = rotated_bias(jobs[r][0], jobs[r][3] // 2)
-                if k >= LAG:
-                    fi, fb0, fnb, fc = jobs[k - LAG]
-                    if (fb0, fc) == (0, 0):
-                        o_new = opool.tile([P, BH, HD], F32, name="o")
-                        outs[fi] = o_new
-                    finish(outs[fi], sums[k - LAG], rbs[(k - LAG) // 2], fc, fb0, fnb, kinds_of(fi)[fc])
-                    if fc == HALF - 1:
-                        for b in range(fb0, fb0 + fnb):
-                            store(outs[fi], fi, b)
-                if k < n_jobs:
-                    size = 2 * DB * H * nb
-                    kind = kinds_of(i)[c]
-                    last_c = max(cc for cc in range(HALF) if kinds_of(i)[cc] != "Y")
-                    if kind == "Y":
-                        x1 = work.tile([P, size], F32, name="xy", bufs=1)
-                        y1 = work.tile([P, size], F32, name="yy", bufs=2)
-                        products(i, c, nb, accs, "Y", x1[:], y1[:])
-                        sums.append(y1[:])
+        for k in range(n_jobs + LAG):
+            if done_perm < HALF:
+                permute(done_perm)
+                done_perm += 1
+            if k < n_jobs:
+                i, b0, nb, c = jobs[k]
+                accs = banks(nb)
+                for s in range(2):
+                    fill(accs[s], i, c, s, b0, nb)
+            r = k - (LAG - 1)
+            if 0 <= r < n_jobs and jobs[r][3] % 2 == 0:
+                rbs[r // 2] = rotated_bias(jobs[r][0], jobs[r][3] // 2)
+            if k >= LAG:
+                fi, fb0, fnb, fc = jobs[k - LAG]
+                if fi not in outs:
+                    if fi % 2 == 0:
+                        o_new = opool.tile([P, BH, HD], F32, name="o0")
                     else:
-                        if place == 0:
-                            x2 = work.tile([P, 2, size], F32, name="x", bufs=3)
-                            y2 = work.tile([P, 2, size], F32, name="y", bufs=LAG // 2 + 2)
-                        products(i, c, nb, accs, kind, x2[:, place], y2[:, place])
-                        sums.append(y2[:, place])
-                        if place == 1 or c == last_c:
-                            eng = nc.vector if k >= n_jobs - 2 else nc.gpsimd
-                            nc_view = slice(0, place + 1)
-                            flat = "p j n -> p (j n)"
-                            eng.tensor_tensor(
-                                out=y2[:, nc_view].rearrange(flat), in0=x2[:, nc_view].rearrange(flat), in1=y2[:, nc_view].rearrange(flat), op=ALU.add
-                            )
-                            place = 0
-                        else:
-                            place = 1
+                        o_new = ovl.tile([P, BH, HD], F32, name="o1", align_bytes=64, offset=0)
+                    outs[fi] = o_new
+                finish(outs[fi], sums[k - LAG], rbs[(k - LAG) // 2], fc, fb0, fnb, kinds_of(fnb)[fc])
+                if fc == HALF - 1:
+                    for b in range(fb0, fb0 + fnb):
+                        store(outs[fi], fi, b)
+            if k < n_jobs:
+                size = 2 * DB * H * nb
+                kind = kinds_of(nb)[c]
+                last_c = max(cc for cc in range(HALF) if kinds_of(nb)[cc] != "Y")
+                if kind == "Y":
+                    x1 = work.tile([P, size], F32, name="xy", bufs=1)
+                    y1 = work.tile([P, size], F32, name="yy", bufs=1)
+                    products(i, c, nb, accs, "Y", x1[:], y1[:])
+                    sums.append(y1[:])
+                else:
+                    if place == 0:
+                        x2 = work.tile([P, 2, size], F32, name="x", bufs=3)
+                        y2 = work.tile([P, 2, size], F32, name="y", bufs=LAG // 2 + 2)
+                    products(i, c, nb, accs, kind, x2[:, place], y2[:, place])
+                    sums.append(y2[:, place])
+                    if place == 1 or c == last_c:
+                        eng = nc.vector if k >= n_jobs - 2 else nc.gpsimd
+                        nc_view = slice(0, place + 1)
+                        flat = "p j n -> p (j n)"
+                        eng.tensor_tensor(
+                            out=y2[:, nc_view].rearrange(flat), in0=x2[:, nc_view].rearrange(flat), in1=y2[:, nc_view].rearrange(flat), op=ALU.add
+                        )
+                        place = 0
+                        state["adds"] += 1
+                        if state["adds"] % NAT_EVERY == 0:
+                            nat_step()
+                    else:
+                        place = 1
+        for rep in range(len(nat_steps)):
+            nat_step()

@@ -30,9 +30,9 @@ X_GROUPS = ((0, 1), (1, 1), (2, 2), (4, 4))
 NAT = ((0, 0),)
 JOBSETS = ((0, 1, 3), (1, 0, 4), (2, 0, 4), (3, 0, 4), (4, 0, 4), (5, 0, 4), (6, 0, 4), (7, 0, 2), (7, 2, 2))
 HG = 8
-NAT_FIRST = 4
+NAT_FIRST = 0
 NAT_EVERY = 1
-PERM_HEAD = 4
+PERM_HEAD = 8
 
 
 def tile_attention_pa_kernel(tc, query_words, query_scales, wq_words, wq_scales, bq, cos, sin, out):
@@ -100,7 +100,7 @@ def tile_attention_pa_kernel(tc, query_words, query_scales, wq_words, wq_scales,
                 nc.tensor.transpose(bt[:, u, :], brow[:, u, :], ident[:])
             nc.scalar.copy(out=bk[:], in_=bt[:, :, 0:H])
             for u in range(2):
-                nc.gpsimd.tensor_tensor(
+                nc.vector.tensor_tensor(
                     out=rr[:, u], in0=mask[:].unsqueeze(2).to_broadcast([P, HH, H]),
                     in1=bk[:, u, :].unsqueeze(1).to_broadcast([P, HH, H]), op=ALU.mult,
                 )

@@ -30,9 +30,7 @@ X_GROUPS = ((0, 1), (1, 1), (2, 2), (4, 4))
 NAT = ((0, 0),)
 JOBSETS = ((0, 1, 3), (1, 0, 4), (2, 0, 4), (3, 0, 4), (4, 0, 4), (5, 0, 4), (6, 0, 4), (7, 0, 2), (7, 2, 2))
 HG = 8
-NAT_FIRST = 0
-NAT_EVERY = 1
-PERM_HEAD = 8
+PERM_FIRST = 3
 
 
 def tile_attention_pa_kernel(tc, query_words, query_scales, wq_words, wq_scales, bq, cos, sin, out):
@@ -127,6 +125,7 @@ def tile_attention_pa_kernel(tc, query_words, query_scales, wq_words, wq_scales,
         nc.vector.memset(xs[:].bitcast(I32), 0)
         nc.scalar.activation(out=warm[:, 1:2], in_=warm[:, 0:1], func=ACT.Copy, scale=1.0)
         make_identity(nc, ident[:])
+        nc.gpsimd.dma_start(out=brow[0:H, 0, :], in_=bq.rearrange("(h d) -> h d", h=H))
         nc.gpsimd.dma_start(out=cs[:], in_=cos.rearrange("a b (i p) d -> p (a b i) d", p=P))
         nc.gpsimd.dma_start(out=sn[:], in_=sin.rearrange("a b (i p) d -> p (a b i) d", p=P))
         qw_v = query_words.rearrange("g p (b w) -> g p b w", b=B)
@@ -155,18 +154,17 @@ def tile_attention_pa_kernel(tc, query_words, query_scales, wq_words, wq_scales,
                     in_=query_scales[:, q : 16 : 4, t0 : t0 + P].rearrange("g r n -> r g n").bitcast(I32),
                 )
 
-        def load_w(g):
-            nc.sync.dma_start(out=wc[:, g].bitcast(I32), in_=wq_words[g].bitcast(I32))
+        def load_w(g0):
+            nc.sync.dma_start(
+                out=wc[:, g0 : g0 + 2].bitcast(I32), in_=wq_words[g0 : g0 + 2].rearrange("g p n -> p g n").bitcast(I32)
+            )
 
-        nc.sync.dma_start(out=brow[0:H, 0, :], in_=bq.rearrange("(h d) -> h d", h=H))
-        load_nat(0)
+        for u in range(n_nat):
+            load_nat(u)
         load_w(0)
+        load_w(2)
         for q in range(4):
             load_scales(ws, wq_scales, q)
-        for g in range(1, PASSES):
-            load_w(g)
-        for u in range(1, n_nat):
-            load_nat(u)
         for q in range(4):
             load_scales(xs, query_scales, q)
         for k in range(len(X_GROUPS)):
@@ -230,25 +228,20 @@ def tile_attention_pa_kernel(tc, query_words, query_scales, wq_words, wq_scales,
                 out=tn[u][:, 4 * j : 4 * j + 4, :], in0=nat_acc[(u, j)][:], in1=bias_bc[:, 4 * j : 4 * j + 4, :], op=ALU.add
             )
 
-        permute(0)
-        done_perm = 1
-        for u in range(n_nat):
-            for j0 in (0, 2):
-                nat_bias(u, j0)
-                nat_bias(u, j0 + 1)
-                if done_perm < PERM_HEAD:
-                    permute(done_perm)
-                    done_perm += 1
-        for c in range(done_perm, PERM_HEAD):
+        for c in range(PERM_FIRST):
             permute(c)
-        done_perm = max(done_perm, PERM_HEAD)
+        for u in range(n_nat):
+            for j in range(4):
+                nat_bias(u, j)
+        for c in range(PERM_FIRST, HALF):
+            permute(c)
 
         nat_steps = []
         for u in range(n_nat):
             for h0 in range(0, H, HG):
                 for part in range(4):
                     nat_steps.append((u, h0, part))
-        state = {"nat": 0, "adds": 0}
+        state = {"nat": 0}
 
         def nat_step():
             if state["nat"] >= len(nat_steps):
@@ -272,8 +265,11 @@ def tile_attention_pa_kernel(tc, query_words, query_scales, wq_words, wq_scales,
                 if h0 + HG == H:
                     nc.sync.dma_start(out=out[b, :, P * i : P * (i + 1), :].rearrange("h p d -> p h d"), in_=tn[u][:])
 
-        for rep in range(NAT_FIRST):
+        def nat_slot():
+            first = state["nat"] < len(nat_steps) and nat_steps[state["nat"]][2] == 0
             nat_step()
+            if first:
+                nat_step()
 
         def fill(view, i, c, s, b0, nb):
             xc_t, li = x_of[i]
@@ -382,9 +378,6 @@ def tile_attention_pa_kernel(tc, query_words, query_scales, wq_words, wq_scales,
             return LAST_KINDS if nb <= 2 else KINDS
 
         for k in range(n_jobs + LAG):
-            if done_perm < HALF:
-                permute(done_perm)
-                done_perm += 1
             if k < n_jobs:
                 i, b0, nb, c = jobs[k]
                 accs = banks(nb)
@@ -428,9 +421,8 @@ def tile_attention_pa_kernel(tc, query_words, query_scales, wq_words, wq_scales,
                             out=y2[:, nc_view].rearrange(flat), in0=x2[:, nc_view].rearrange(flat), in1=y2[:, nc_view].rearrange(flat), op=ALU.add
                         )
                         place = 0
-                        state["adds"] += 1
-                        if state["adds"] % NAT_EVERY == 0:
-                            nat_step()
+                        if c + 1 < HALF and kinds_of(nb)[c + 1] == "Y":
+                            nat_slot()
                     else:
                         place = 1
         for rep in range(len(nat_steps)):

@@ -41,11 +41,16 @@ def tile_attention_pa_kernel(tc, query_words, query_scales, wq_words, wq_scales,
         ovl = ctx.enter_context(tc.tile_pool(name="ovl", bufs=1))
         opool = ctx.enter_context(tc.tile_pool(name="opool", bufs=1))
         work = ctx.enter_context(tc.tile_pool(name="work", bufs=4))
+        late = ctx.enter_context(tc.tile_pool(name="late", bufs=1))
         psum = ctx.enter_context(tc.psum_pool(name="psum", bufs=6))
         psc = ctx.enter_context(tc.psum_pool(name="psc", bufs=2))
         ctx.enter_context(tc.manual_schedule())
 
         xs = keep.tile([P, PASSES, B * S], U8, align_bytes=64)
+        tn = []
+        for u in range(n_nat):
+            tn_t = keep.tile([P, H, HD], F32, name="tn%d" % u)
+            tn.append(tn_t)
         cf = keep.tile([P, NT, HD], F32)
         sg = keep.tile([P, NT, HD], F32)
         lt = keep.tile([P, NT, 2, P], BF16)
@@ -55,14 +60,10 @@ def tile_attention_pa_kernel(tc, query_words, query_scales, wq_words, wq_scales,
         brow = keep.tile([P, 2, P], BF16)
         bk = keep.tile([P, 2, H], BF16)
         warm = keep.tile([P, 2], F32)
-        bias_bc = keep.tile([P, H, HD], BF16)
-        xn = keep.tile([P, n_nat, PASSES, 2 * P], U8, align_bytes=64)
-        xsn = keep.tile([P, n_nat, PASSES, P], U8, align_bytes=64)
-        yn = keep.tile([P, HG, HD], F32)
-        tn = []
-        for u in range(n_nat):
-            tn_t = keep.tile([P, H, HD], F32, name="tn%d" % u)
-            tn.append(tn_t)
+        bias_bc = late.tile([P, H, HD], BF16)
+        xn = late.tile([P, n_nat, PASSES, 2 * P], U8, align_bytes=64)
+        xsn = late.tile([P, n_nat, PASSES, P], U8, align_bytes=64)
+        yn = late.tile([P, HG, HD], F32)
         x_of = {}
         x_tiles = []
         for i0, n in X_GROUPS:
@@ -389,10 +390,10 @@ def tile_attention_pa_kernel(tc, query_words, query_scales, wq_words, wq_scales,
             if k >= LAG:
                 fi, fb0, fnb, fc = jobs[k - LAG]
                 if fi not in outs:
-                    if fi % 2 == 0:
-                        o_new = opool.tile([P, BH, HD], F32, name="o0")
+                    if fi % 2 == 1:
+                        o_new = opool.tile([P, BH, HD], F32, name="o1")
                     else:
-                        o_new = ovl.tile([P, BH, HD], F32, name="o1", align_bytes=64, offset=0)
+                        o_new = ovl.tile([P, BH, HD], F32, name="o0", align_bytes=64, offset=0)
                     outs[fi] = o_new
                 finish(outs[fi], sums[k - LAG], rbs[(k - LAG) // 2], fc, fb0, fnb, kinds_of(fnb)[fc])
                 if fc == HALF - 1:
@@ -404,7 +405,7 @@ def tile_attention_pa_kernel(tc, query_words, query_scales, wq_words, wq_scales,
                 last_c = max(cc for cc in range(HALF) if kinds_of(nb)[cc] != "Y")
                 if kind == "Y":
                     x1 = work.tile([P, size], F32, name="xy", bufs=1)
-                    y1 = work.tile([P, size], F32, name="yy", bufs=1)
+                    y1 = work.tile([P, size], F32, name="yy", bufs=2)
                     products(i, c, nb, accs, "Y", x1[:], y1[:])
                     sums.append(y1[:])
                 else:

@@ -124,11 +124,11 @@ def tile_attention_pa_kernel(tc, query_words, query_scales, wq_words, wq_scales,
         nc.vector.memset(xsn[:].rearrange("p u g n -> p (u g n)").bitcast(I32), 0)
         nc.vector.memset(ws[:].bitcast(I32), 0)
         nc.vector.memset(xs[:].bitcast(I32), 0)
+        nc.scalar.dma_start(out=cs[:], in_=cos.rearrange("a b (i p) d -> p (a b i) d", p=P))
+        nc.scalar.dma_start(out=sn[:], in_=sin.rearrange("a b (i p) d -> p (a b i) d", p=P))
         nc.scalar.activation(out=warm[:, 1:2], in_=warm[:, 0:1], func=ACT.Copy, scale=1.0)
         make_identity(nc, ident[:])
         nc.gpsimd.dma_start(out=brow[0:H, 0, :], in_=bq.rearrange("(h d) -> h d", h=H))
-        nc.gpsimd.dma_start(out=cs[:], in_=cos.rearrange("a b (i p) d -> p (a b i) d", p=P))
-        nc.gpsimd.dma_start(out=sn[:], in_=sin.rearrange("a b (i p) d -> p (a b i) d", p=P))
         qw_v = query_words.rearrange("g p (b w) -> g p b w", b=B)
 
         def load_x(k):

@@ -27,8 +27,8 @@ KINDS = ("Z", "N", "Z", "Z", "N", "Z", "Y", "Z")
 LAST_KINDS = ("Z", "N", "Z", "N", "Z", "N", "Z", "N")
 LAG = 5
 X_GROUPS = ((0, 1), (1, 1), (2, 2), (4, 4))
-NAT = ((0, 0),)
-JOBSETS = ((0, 1, 3), (1, 0, 4), (2, 0, 4), (3, 0, 4), (4, 0, 4), (5, 0, 4), (6, 0, 4), (7, 0, 2), (7, 2, 2))
+NAT = ((7, 3),)
+JOBSETS = ((0, 0, 4), (1, 0, 4), (2, 0, 4), (3, 0, 4), (4, 0, 4), (5, 0, 4), (6, 0, 4), (7, 0, 2), (7, 2, 1))
 HG = 8
 PERM_FIRST = 3
 
@@ -98,6 +98,8 @@ def tile_attention_pa_kernel(tc, query_words, query_scales, wq_words, wq_scales,
             for u in range(2):
                 nc.tensor.transpose(bt[:, u, :], brow[:, u, :], ident[:])
             nc.scalar.copy(out=bk[:], in_=bt[:, :, 0:H])
+
+        def bias_diagonal():
             for u in range(2):
                 nc.vector.tensor_tensor(
                     out=rr[:, u], in0=mask[:].unsqueeze(2).to_broadcast([P, HH, H]),
@@ -174,14 +176,16 @@ def tile_attention_pa_kernel(tc, query_words, query_scales, wq_words, wq_scales,
         nc.vector.tensor_tensor(out=mask[:], in0=ident[:, 0:HH], in1=ident[:, HH:P], op=ALU.add)
         nc.vector.tensor_copy(out=brow[:, 1, 0:HH], in_=brow[:, 0, HH:HD])
         nc.vector.tensor_copy(out=brow[:, 1, HH:HD], in_=brow[:, 0, 0:HH])
-        bias_rows()
-        bias_table()
         cs_v = cs[:].rearrange("p i (u d) -> p i u d", u=2)
         sn_v = sn[:].rearrange("p i (u d) -> p i u d", u=2)
         sg_v = sg[:].rearrange("p i (u d) -> p i u d", u=2)
         nc.scalar.copy(out=csall[:, :, :, 0, :], in_=cs_v)
         nc.scalar.activation(out=csall[:, :, 0, 1, :], in_=sn_v[:, :, 0, :], func=ACT.Copy, scale=-1.0)
         nc.scalar.copy(out=csall[:, :, 1, 1, :], in_=sn_v[:, :, 1, :])
+        turn_tables(0, psum, "acc")
+        turn_tables(2, psum, "acc")
+        bias_rows()
+        bias_table()
         for tiles in (slice(0, 1), slice(1, NT)):
             nc.scalar.copy(out=cf[:, tiles], in_=cs[:, tiles])
             nc.scalar.activation(out=sg_v[:, tiles, 0, :], in_=sn_v[:, tiles, 0, :], func=ACT.Copy, scale=-1.0)
@@ -211,8 +215,6 @@ def tile_attention_pa_kernel(tc, query_words, query_scales, wq_words, wq_scales,
                     for j in range(4):
                         nat_pass(nat_acc[(0, j)], 0, j, g)
 
-        turn_tables(0, psum, "acc")
-        turn_tables(2, psum, "acc")
         turn_tables(4, psc, "cps")
         turn_tables(6, psc, "cps")
 
@@ -236,6 +238,7 @@ def tile_attention_pa_kernel(tc, query_words, query_scales, wq_words, wq_scales,
                 nat_bias(u, j)
         for c in range(PERM_FIRST, HALF):
             permute(c)
+        bias_diagonal()
 
         nat_steps = []
         for u in range(n_nat):

from contextlib import ExitStack

import concourse.mybir as mybir
from concourse.masks import make_identity

F32 = mybir.dt.float32
BF16 = mybir.dt.bfloat16
U8 = mybir.dt.uint8
I32 = mybir.dt.int32
FP4 = mybir.dt.float4_e2m1fn_x4
ALU = mybir.AluOpType
ACT = mybir.ActivationFunctionType

B, S, DIM, H, HD = 4, 1024, 2048, 16, 128
E = H * HD
P = 128
PASSES = DIM // 512
NT = S // P
DB = 8
NBLK = HD // DB
HALF = NBLK // 2
HH = HD // 2
BH = B * H
FLOPS = 2 * B * S * DIM * E

KINDS = ("Z", "N", "Z", "Z", "N", "Z", "Y", "Z")
LAST_KINDS = ("Z", "N", "Z", "N", "Z", "N", "Z", "N")
LAG = 5
X_GROUPS = ((0, 1), (1, 1), (2, 2), (4, 4))
NAT = ((7, 3),)
JOBSETS = ((0, 0, 4), (1, 0, 4), (2, 0, 4), (3, 0, 4), (4, 0, 4), (5, 0, 4), (6, 0, 4), (7, 0, 2), (7, 2, 1))
HG = 8
PERM_FIRST = 3


def tile_attention_pa_kernel(tc, query_words, query_scales, wq_words, wq_scales, bq, cos, sin, out):
    nc = tc.nc
    n_nat = len(NAT)
    with ExitStack() as ctx:
        keep = ctx.enter_context(tc.tile_pool(name="keep", bufs=1))
        ovl = ctx.enter_context(tc.tile_pool(name="ovl", bufs=1))
        opool = ctx.enter_context(tc.tile_pool(name="opool", bufs=1))
        work = ctx.enter_context(tc.tile_pool(name="work", bufs=4))
        late = ctx.enter_context(tc.tile_pool(name="late", bufs=1))
        psum = ctx.enter_context(tc.psum_pool(name="psum", bufs=6))
        psc = ctx.enter_context(tc.psum_pool(name="psc", bufs=2))
        ctx.enter_context(tc.manual_schedule())

        xs = keep.tile([P, PASSES, B * S], U8, align_bytes=64)
        tn = []
        for u in range(n_nat):
            tn_t = keep.tile([P, H, HD], F32, name="tn%d" % u)
            tn.append(tn_t)
        cf = keep.tile([P, NT, HD], F32)
        sg = keep.tile([P, NT, HD], F32)
        lt = keep.tile([P, NT, 2, P], BF16)
        rr = keep.tile([P, 2, HH, H], BF16)
        ident = keep.tile([P, P], BF16)
        mask = keep.tile([P, HH], BF16)
        brow = keep.tile([P, 2, P], BF16)
        bk = keep.tile([P, 2, H], BF16)
        warm = keep.tile([P, 2], F32)
        bias_bc = late.tile([P, H, HD], BF16)
        xn = late.tile([P, n_nat, PASSES, 2 * P], U8, align_bytes=64)
        xsn = late.tile([P, n_nat, PASSES, P], U8, align_bytes=64)
        yn = late.tile([P, HG, HD], F32)
        x_of = {}
        x_tiles = []
        for i0, n in X_GROUPS:
            xc_t = keep.tile([P, PASSES, B, 2 * P * n], U8, align_bytes=64, name="xc%d" % i0)
            x_tiles.append(xc_t)
            for i in range(i0, i0 + n):
                x_of[i] = (xc_t, i - i0)
        w_c, w_s = [], []
        for c in range(HALF):
            w_c_t = keep.tile([P, PASSES, 2, 2 * P], U8, align_bytes=64, name="wc%d" % c)
            w_s_t = keep.tile([P, PASSES, 2, P], U8, align_bytes=64, name="ws%d" % c)
            w_c.append(w_c_t)
            w_s.append(w_s_t)
        wc = ovl.tile([P, PASSES, 2 * E], U8, align_bytes=64, offset=0)
        ws = ovl.tile([P, PASSES, E], U8, align_bytes=64, offset=16384)
        cs = ovl.tile([P, NT, HD], BF16, align_bytes=64, offset=24576)
        sn = ovl.tile([P, NT, HD], BF16, align_bytes=64, offset=26624)
        csall = ovl.tile([P, NT, 2, 2, HH], BF16, align_bytes=64, offset=28672)

        def bias_rows():
            for j in range(4):
                bb = psum.tile([P, 4, HD], F32, name="acc")
                for h4 in range(4):
                    h = 4 * j + h4
                    nc.tensor.matmul(
                        out=bb[:, h4, :], lhsT=ident[:, h : h + 1].to_broadcast([P, P]), rhs=brow[:, 0, :], start=True, stop=True
                    )
                nc.scalar.copy(out=bias_bc[:, 4 * j : 4 * j + 4, :], in_=bb[:])

        def bias_table():
            bt = psc.tile([P, 2, P], BF16, name="cps")
            for u in range(2):
                nc.tensor.transpose(bt[:, u, :], brow[:, u, :], ident[:])
            nc.scalar.copy(out=bk[:], in_=bt[:, :, 0:H])

        def bias_diagonal():
            for u in range(2):
                nc.vector.tensor_tensor(
                    out=rr[:, u], in0=mask[:].unsqueeze(2).to_broadcast([P, HH, H]),
                    in1=bk[:, u, :].unsqueeze(1).to_broadcast([P, HH, H]), op=ALU.mult,
                )

        def turn_tables(i0, pool, tag):
            tp = pool.tile([P, 4, P], BF16, name=tag)
            for j in range(4):
                nc.tensor.transpose(tp[:, j, :], csall[:, i0 + j // 2, j % 2].rearrange("p k d -> p (k d)"), ident[:])
            nc.scalar.copy(out=lt[:, i0 : i0 + 2].rearrange("p i u t -> p (i u) t"), in_=tp[:])

        def rotated_bias(i, m):
            rb = psc.tile([P, 2, 2 * DB, H], F32, name="cps")
            for u in range(2):
                nc.tensor.matmul(
                    out=rb[:, u].rearrange("p d h -> p (d h)"), lhsT=lt[:, i, u, :],
                    rhs=rr[:, u, 2 * DB * m : 2 * DB * (m + 1), :].rearrange("p d h -> p (d h)"), start=True, stop=True,
                )
            return rb

        nc.vector.memset(brow[:, 0, :], 0.0)
        nc.vector.memset(warm[:, 0:1], 0.0)
        nc.vector.memset(xsn[:].rearrange("p u g n -> p (u g n)").bitcast(I32), 0)
        nc.vector.memset(ws[:].bitcast(I32), 0)
        nc.vector.memset(xs[:].bitcast(I32), 0)
        nc.scalar.dma_start(out=cs[:], in_=cos.rearrange("a b (i p) d -> p (a b i) d", p=P))
        nc.scalar.dma_start(out=sn[:], in_=sin.rearrange("a b (i p) d -> p (a b i) d", p=P))
        nc.scalar.activation(out=warm[:, 1:2], in_=warm[:, 0:1], func=ACT.Copy, scale=1.0)
        make_identity(nc, ident[:])
        nc.gpsimd.dma_start(out=brow[0:H, 0, :], in_=bq.rearrange("(h d) -> h d", h=H))
        qw_v = query_words.rearrange("g p (b w) -> g p b w", b=B)

        def load_x(k):
            i0, n = X_GROUPS[k]
            for g in range(PASSES):
                nc.sync.dma_start(
                    out=x_tiles[k][:, g].bitcast(I32), in_=qw_v[g, :, :, 2 * P * i0 : 2 * P * (i0 + n)].bitcast(I32)
                )

        def load_scales(plane, rows, q):
            nc.sync.dma_start(
                out=plane[q : P : 32, :, :].bitcast(I32),
                in_=rows[:, q : 16 : 4, :].rearrange("g r n -> r g n").bitcast(I32),
            )

        def load_nat(u):
            t0 = NAT[u][1] * S + NAT[u][0] * P
            nc.sync.dma_start(
                out=xn[:, u].bitcast(I32), in_=query_words[:, :, 2 * t0 : 2 * (t0 + P)].rearrange("g p w -> p g w").bitcast(I32)
            )
            for q in range(4):
                nc.sync.dma_start(
                    out=xsn[q : P : 32, u].bitcast(I32),
                    in_=query_scales[:, q : 16 : 4, t0 : t0 + P].rearrange("g r n -> r g n").bitcast(I32),
                )

        def load_w(g0):
            nc.sync.dma_start(
                out=wc[:, g0 : g0 + 2].bitcast(I32), in_=wq_words[g0 : g0 + 2].rearrange("g p n -> p g n").bitcast(I32)
            )

        for u in range(n_nat):
            load_nat(u)
        load_w(0)
        load_w(2)
        for q in range(4):
            load_scales(ws, wq_scales, q)
        for q in range(4):
            load_scales(xs, query_scales, q)
        for k in range(len(X_GROUPS)):
            load_x(k)

        nc.vector.tensor_tensor(out=mask[:], in0=ident[:, 0:HH], in1=ident[:, HH:P], op=ALU.add)
        nc.vector.tensor_copy(out=brow[:, 1, 0:HH], in_=brow[:, 0, HH:HD])
        nc.vector.tensor_copy(out=brow[:, 1, HH:HD], in_=brow[:, 0, 0:HH])
        cs_v = cs[:].rearrange("p i (u d) -> p i u d", u=2)
        sn_v = sn[:].rearrange("p i (u d) -> p i u d", u=2)
        sg_v = sg[:].rearrange("p i (u d) -> p i u d", u=2)
        nc.scalar.copy(out=csall[:, :, :, 0, :], in_=cs_v)
        nc.scalar.activation(out=csall[:, :, 0, 1, :], in_=sn_v[:, :, 0, :], func=ACT.Copy, scale=-1.0)
        nc.scalar.copy(out=csall[:, :, 1, 1, :], in_=sn_v[:, :, 1, :])
        turn_tables(0, psum, "acc")
        turn_tables(2, psum, "acc")
        bias_rows()
        bias_table()
        for tiles in (slice(0, 1), slice(1, NT)):
            nc.scalar.copy(out=cf[:, tiles], in_=cs[:, tiles])
            nc.scalar.activation(out=sg_v[:, tiles, 0, :], in_=sn_v[:, tiles, 0, :], func=ACT.Copy, scale=-1.0)
            nc.scalar.copy(out=sg_v[:, tiles, 1, :], in_=sn_v[:, tiles, 1, :])

        def nat_pass(acc, u, j, g):
            nc.tensor.matmul_mx(
                out=acc[:].rearrange("p h d -> p (h d)"),
                lhsT=xn[:, u, g, :].bitcast(FP4),
                lhsT_scale=xsn[:, u, g, :],
                rhs=wc[:, g, 1024 * j : 1024 * (j + 1)].bitcast(FP4),
                rhs_scale=ws[:, g, 512 * j : 512 * (j + 1)],
                start=(g == 0),
                stop=(g == PASSES - 1),
            )

        nat_acc = {}
        for u in range(n_nat):
            for j in range(4):
                acc_n = psum.tile([P, 4, HD], F32, name="acc")
                nat_acc[(u, j)] = acc_n
                if u > 0:
                    for g in range(PASSES):
                        nat_pass(acc_n, u, j, g)
            if u == 0:
                for g in range(PASSES):
                    for j in range(4):
                        nat_pass(nat_acc[(0, j)], 0, j, g)

        turn_tables(4, psc, "cps")
        turn_tables(6, psc, "cps")

        def permute(c):
            for src, dst, w in ((ws, w_s, 2), (wc, w_c, 4)):
                for s in range(2):
                    nc.vector.tensor_copy(
                        out=dst[c][:, :, s, :].bitcast(I32).rearrange("p g (h w) -> p g h w", h=H),
                        in_=src[:].bitcast(I32).rearrange("p g (h s c w) -> p g s c h w", h=H, s=2, w=w)[:, :, s, c],
                    )

        def nat_bias(u, j):
            nc.vector.tensor_tensor(
                out=tn[u][:, 4 * j : 4 * j + 4, :], in0=nat_acc[(u, j)][:], in1=bias_bc[:, 4 * j : 4 * j + 4, :], op=ALU.add
            )

        for c in range(PERM_FIRST):
            permute(c)
        for u in range(n_nat):
            for j in range(4):
                nat_bias(u, j)
        for c in range(PERM_FIRST, HALF):
            permute(c)
        bias_diagonal()

        nat_steps = []
        for u in range(n_nat):
            for h0 in range(0, H, HG):
                for part in range(4):
                    nat_steps.append((u, h0, part))
        state = {"nat": 0}

        def nat_step():
            if state["nat"] >= len(nat_steps):
                return
            u, h0, part = nat_steps[state["nat"]]
            state["nat"] += 1
            i, b = NAT[u]
            tv = tn[u][:, h0 : h0 + HG, :]
            if part == 0:
                nc.gpsimd.tensor_tensor(
                    out=yn[:, :, 0:HH], in0=tv[:, :, HH:HD], in1=sg[:, i, 0:HH].unsqueeze(1).to_broadcast([P, HG, HH]), op=ALU.mult
                )
            elif part == 1:
                nc.gpsimd.tensor_tensor(
                    out=yn[:, :, HH:HD], in0=tv[:, :, 0:HH], in1=sg[:, i, HH:HD].unsqueeze(1).to_broadcast([P, HG, HH]), op=ALU.mult
                )
            elif part == 2:
                nc.gpsimd.tensor_tensor(out=tv, in0=tv, in1=cf[:, i, :].unsqueeze(1).to_broadcast([P, HG, HD]), op=ALU.mult)
            else:
                nc.gpsimd.tensor_tensor(out=tv, in0=tv, in1=yn[:], op=ALU.add)
                if h0 + HG == H:
                    nc.sync.dma_start(out=out[b, :, P * i : P * (i + 1), :].rearrange("h p d -> p h d"), in_=tn[u][:])

        def nat_slot():
            first = state["nat"] < len(nat_steps) and nat_steps[state["nat"]][2] == 0
            nat_step()
            if first:
                nat_step()

        def fill(view, i, c, s, b0, nb):
            xc_t, li = x_of[i]
            for j in range(nb):
                t0 = (b0 + j) * S + i * P
                for g in range(PASSES):
                    nc.tensor.matmul_mx(
                        out=view[:, j].rearrange("p h e -> p (h e)"),
                        lhsT=xc_t[:, g, b0 + j, 2 * P * li : 2 * P * (li + 1)].bitcast(FP4),
                        lhsT_scale=xs[:, g, t0 : t0 + P],
                        rhs=w_c[c][:, g, s, :].bitcast(FP4),
                        rhs_scale=w_s[c][:, g, s, :],
                        start=(g == 0),
                        stop=(g == PASSES - 1),
                    )

        def banks(nb):
            if 2 * nb * P > 512:
                acc_lo = psum.tile([P, nb, H, DB], F32, name="acc")
                acc_hi = psum.tile([P, nb, H, DB], F32, name="acc")
                return (acc_lo[:], acc_hi[:])
            acc2 = psum.tile([P, 2, nb, H, DB], F32, name="acc")
            return (acc2[:, 0], acc2[:, 1])

        def products(i, c, nb, accs, kind, xf, yf):
            if kind == "Y":
                x = xf.rearrange("p (s e h b) -> p s e h b", s=2, e=DB, h=H)
                y = yf.rearrange("p (s e h b) -> p s e h b", s=2, e=DB, h=H)
                for s in range(2):
                    for e in range(DB):
                        d = DB * (c + HALF * s) + e
                        nc.scalar.activation(
                            out=x[:, s, e], in_=accs[s][:, :, :, e].rearrange("p b h -> p h b"), func=ACT.Copy,
                            scale=cf[:, i, d : d + 1],
                        )
                for s in range(2):
                    for e in range(DB):
                        d = DB * (c + HALF * s) + e
                        nc.vector.scalar_tensor_tensor(
                            out=y[:, s, e], in0=accs[1 - s][:, :, :, e].rearrange("p b h -> p h b"), scalar=sg[:, i, d : d + 1],
                            in1=x[:, s, e], op0=ALU.mult, op1=ALU.add,
                        )
            elif kind == "Z":
                x = xf.rearrange("p (s e h b) -> p s e h b", s=2, e=DB, h=H)
                y = yf.rearrange("p (s e h b) -> p s e h b", s=2, e=DB, h=H)
                for t in range(2):
                    for s, dst, tab in ((t, x, cf), (1 - t, y, sg)):
                        for e in range(DB):
                            d = DB * (c + HALF * s) + e
                            nc.scalar.activation(
                                out=dst[:, s, e], in_=accs[t][:, :, :, e].rearrange("p b h -> p h b"), func=ACT.Copy,
                                scale=tab[:, i, d : d + 1],
                            )
            else:
                x = xf.rearrange("p (s n e) -> p s n e", s=2, e=DB)
                y = yf.rearrange("p (s n e) -> p s n e", s=2, e=DB)
                for t in range(2):
                    for s, dst, tab in ((t, x, cf), (1 - t, y, sg)):
                        d0 = DB * (c + HALF * s)
                        nc.vector.tensor_tensor(
                            out=dst[:, s], in0=accs[t].rearrange("p b h e -> p (b h) e"),
                            in1=tab[:, i, d0 : d0 + DB].unsqueeze(1).to_broadcast([P, nb * H, DB]), op=ALU.mult,
                        )

        def finish(o, yf, rb, c, b0, nb, kind):
            if kind != "N":
                y = yf.rearrange("p (s e h b) -> p s e h b", s=2, e=DB, h=H)
            else:
                y = yf.rearrange("p (s b h e) -> p s b h e", s=2, h=H, e=DB)
            rows = o[:, H * b0 : H * (b0 + nb), :]
            e0 = DB * (c % 2)
            for s in range(2):
                d0 = DB * (c + HALF * s)
                if kind != "N":
                    for u in range(2):
                        nc.vector.tensor_tensor(
                            out=rows[:, :, d0 + 4 * u : d0 + 4 * u + 4].rearrange("p (b h) e -> p h b e", h=H),
                            in0=y[:, s, 4 * u : 4 * u + 4].rearrange("p e h b -> p h b e"),
                            in1=rb[:, s, e0 + 4 * u : e0 + 4 * u + 4, :].rearrange("p e h -> p h e").unsqueeze(2).to_broadcast([P, H, nb, 4]),
                            op=ALU.add,
                        )
                else:
                    nc.vector.tensor_tensor(
                        out=rows[:, :, d0 : d0 + DB].rearrange("p (b h) e -> p b h e", h=H),
                        in0=y[:, s],
                        in1=rb[:, s, e0 : e0 + DB, :].rearrange("p e h -> p h e").unsqueeze(1).to_broadcast([P, nb, H, DB]),
                        op=ALU.add,
                    )

        def store(o, i, b):
            nc.sync.dma_start(
                out=out[b, :, P * i : P * (i + 1), :].rearrange("h p d -> p h d"), in_=o[:, H * b : H * (b + 1), :]
            )

        jobs = []
        for i, b0, nb in JOBSETS:
            for c in range(HALF):
                jobs.append((i, b0, nb, c))
        n_jobs = len(jobs)
        outs = {}
        sums = []
        rbs = {}
        place = 0

        def kinds_of(nb):
            return LAST_KINDS if nb <= 2 else KINDS

        for k in range(n_jobs + LAG):
            if k < n_jobs:
                i, b0, nb, c = jobs[k]
                accs = banks(nb)
                for s in range(2):
                    fill(accs[s], i, c, s, b0, nb)
            r = k - (LAG - 1)
            if 0 <= r < n_jobs and jobs[r][3] % 2 == 0:
                rbs[r // 2] = rotated_bias(jobs[r][0], jobs[r][3] // 2)
            if k >= LAG:
                fi, fb0, fnb, fc = jobs[k - LAG]
                if fi not in outs:
                    if fi % 2 == 1:
                        o_new = opool.tile([P, BH, HD], F32, name="o1")
                    else:
                        o_new = ovl.tile([P, BH, HD], F32, name="o0", align_bytes=64, offset=0)
                    outs[fi] = o_new
                finish(outs[fi], sums[k - LAG], rbs[(k - LAG) // 2], fc, fb0, fnb, kinds_of(fnb)[fc])
                if fc == HALF - 1:
                    for b in range(fb0, fb0 + fnb):
                        store(outs[fi], fi, b)
            if k < n_jobs:
                size = 2 * DB * H * nb
                kind = kinds_of(nb)[c]
                last_c = max(cc for cc in range(HALF) if kinds_of(nb)[cc] != "Y")
                if kind == "Y":
                    x1 = work.tile([P, size], F32, name="xy", bufs=1)
                    y1 = work.tile([P, size], F32, name="yy", bufs=2)
                    products(i, c, nb, accs, "Y", x1[:], y1[:])
                    sums.append(y1[:])
                else:
                    if place == 0:
                        x2 = work.tile([P, 2, size], F32, name="x", bufs=3)
                        y2 = work.tile([P, 2, size], F32, name="y", bufs=LAG // 2 + 2)
                    products(i, c, nb, accs, kind, x2[:, place], y2[:, place])
                    sums.append(y2[:, place])
                    if place == 1 or c == last_c:
                        eng = nc.vector if k >= n_jobs - 2 else nc.gpsimd
                        nc_view = slice(0, place + 1)
                        flat = "p j n -> p (j n)"
                        eng.tensor_tensor(
                            out=y2[:, nc_view].rearrange(flat), in0=x2[:, nc_view].rearrange(flat), in1=y2[:, nc_view].rearrange(flat), op=ALU.add
                        )
                        place = 0
                        if c + 1 < HALF and kinds_of(nb)[c + 1] == "Y":
                            nat_slot()
                    else:
                        place = 1
        for rep in range(len(nat_steps)):
            nat_step()
